import numpy as np
import ml_dtypes


def mxq(x, axis, fmt="e4m3"):
    dtype, down = {"e4m3": (ml_dtypes.float8_e4m3fn, 7), "e5m2": (ml_dtypes.float8_e5m2, 14)}[fmt]
    v = np.moveaxis(np.asarray(x, np.float32).astype(ml_dtypes.bfloat16).astype(np.float64), axis, -1)
    blocks = v.reshape(v.shape[:-1] + (-1, 32))
    amax = np.abs(blocks).max(-1, keepdims=True)
    byte = np.maximum(np.where(amax > 0, np.frexp(amax)[1] - 1 + 127, 0) - down, 1)
    scale = np.exp2(byte - 127.0)
    codes = (blocks / scale).astype(np.float32).astype(dtype).astype(np.float64)
    return np.moveaxis((codes * scale).reshape(v.shape), -1, axis)


WIDE = False


def mx_kscale(k):
    if not WIDE:
        return np.ones(k)
    levels = np.array([10, -10, 5, -5, 0])
    a = np.random.permutation(np.resize(levels, k // 512 * 4)).reshape(k // 512, 4)
    idx = np.arange(k)
    return np.exp2(a[idx // 512, idx % 128 // 32])


BF16 = ml_dtypes.bfloat16


def bf(x):
    return np.asarray(x, np.float32).astype(BF16)


def f64(x):
    return np.asarray(x).astype(np.float64)


B, N, H, DH, E, W, DQ, DKV = 8, 512, 4, 128, 2, 128, 1024, 512
DV = E * DH
DM = H * DV
NEG = -3.4028234663852886e38


def silu(v):
    return v / (1.0 + np.exp(-v))


def split_heads(t):
    return t.reshape(B, N, H, DV).transpose(0, 2, 1, 3)


def setup_inputs():
    s = mx_kscale(DKV)
    return {"q": bf(np.random.standard_normal((B, H, N, DH)) * 1.4),
            "k1": bf(np.random.standard_normal((B, H, N, DH)) * 1.4),
            "key_values_input": bf(np.random.standard_normal((B, N, DKV)) * s),
            "Wv1": bf(np.random.standard_normal((DKV, DM)) * 4.0 / np.sqrt(DKV) / s[:, None]),
            "attn_sink": bf(np.log(N) + 0.5 + 0.5 * np.random.standard_normal(H))}


def reference(q, k1, key_values_input, Wv1, attn_sink):
    v1 = split_heads(mxq(f64(key_values_input), 2, "e4m3") @ mxq(f64(Wv1), 0, "e4m3"))
    sim = f64(q) @ f64(k1).transpose(0, 1, 3, 2) * DH ** -0.5
    idx = np.arange(N)
    mask = (idx[None, :] > idx[:, None]) & (idx[None, :] - idx[:, None] <= W)
    sim = np.where(mask, NEG, sim)
    sink = f64(attn_sink)[None, :, None, None]
    m = np.maximum(sim.max(-1, keepdims=True), sink)
    e = np.exp(sim - m)
    den = e.sum(-1, keepdims=True) + np.exp(sink - m)
    return silu((mxq(e, 3, "e4m3") @ mxq(v1, 2, "e4m3")) / den)

@@ -1,0 +1,315 @@
+from contextlib import ExitStack
+
+import concourse.mybir as mybir
+from concourse.masks import make_identity
+
+F32 = mybir.dt.float32
+BF16 = mybir.dt.bfloat16
+U32 = mybir.dt.uint32
+U8 = mybir.dt.uint8
+FP8X4 = mybir.dt.float8_e4m3fn_x4
+ACT = mybir.ActivationFunctionType
+ALU = mybir.AluOpType
+
+B, H, N, DH = 8, 4, 512, 128
+DV = 256
+DKV = 512
+DM = H * DV
+P = 128
+PACK = 4
+TILES = N // P
+CHUNKS = DM // P
+UNITS = B * H
+GROUP_BATCHES = 2
+GROUP = GROUP_BATCHES * H
+SCALE = DH**-0.5
+NEG = -3.4028234663852886e38
+
+FLOPS = 2 * B * N * DKV * DM + 2 * UNITS * N * N * DH + 2 * UNITS * N * N * DV
+
+
+def tile_attention_pa_t_kernel(tc, q, k1, key_values_input, Wv1, attn_sink, out):
+    nc = tc.nc
+    with ExitStack() as stack:
+        stack.enter_context(tc.manual_schedule())
+
+        const = stack.enter_context(tc.tile_pool(name="const", bufs=1))
+        qk_in = stack.enter_context(tc.tile_pool(name="qk_in", bufs=3))
+        kv_in = stack.enter_context(tc.tile_pool(name="kv_in", bufs=3))
+        turned_qk = stack.enter_context(tc.tile_pool(name="turned_qk", bufs=2))
+        e_pool = stack.enter_context(tc.tile_pool(name="e_pool", bufs=3))
+        scratch = stack.enter_context(tc.tile_pool(name="scratch", bufs=4))
+        stats = stack.enter_context(tc.tile_pool(name="stats", bufs=GROUP + 4))
+        grouped = stack.enter_context(tc.tile_pool(name="grouped", bufs=2))
+        e_mx = stack.enter_context(tc.tile_pool(name="e_mx", bufs=GROUP + 2))
+        kv_mx = stack.enter_context(tc.tile_pool(name="kv_mx", bufs=GROUP_BATCHES))
+        v_mx = stack.enter_context(tc.tile_pool(name="v_mx", bufs=2 * GROUP_BATCHES))
+        results = stack.enter_context(tc.tile_pool(name="results", bufs=3))
+        ps_s = stack.enter_context(tc.psum_pool(name="ps_s", bufs=4))
+        ps_x = stack.enter_context(tc.psum_pool(name="ps_x", bufs=4))
+
+        q_sb, k_sb, kv_sb = {}, {}, {}
+        kv_grouped, kv_codes, kv_scales = {}, {}, {}
+        v_grouped, v_codes, v_scales = {}, {}, {}
+        qkT, e_sb, e_grouped, e_codes, e_scales = {}, {}, {}, {}, {}
+        neg_max, row_sum, sink_e, rden = {}, {}, {}, {}
+
+        def load_qk(b):
+            q_sb[b] = qk_in.tile([P, H, TILES, DH], BF16, name="q_sb")
+            k_sb[b] = qk_in.tile([P, H, TILES, DH], BF16, name="k_sb")
+            nc.sync.dma_start(out=q_sb[b][:], in_=q[b].rearrange("h (a p) d -> p h a d", p=P))
+            nc.sync.dma_start(out=k_sb[b][:], in_=k1[b].rearrange("h (a p) d -> p h a d", p=P))
+
+        def load_kv(b):
+            kv_sb[b] = kv_in.tile([P, PACK, DKV], BF16, name="kv_sb")
+            nc.sync.dma_start(
+                out=kv_sb[b][:].rearrange("p (w e) f -> p w (e f)", w=2),
+                in_=key_values_input[b].rearrange("(w p e) f -> p w (e f)", w=2, e=2),
+            )
+
+        def regroup_by_transposes(words, target, copies):
+            target_words = target[:].bitcast(F32)
+            for half in range(2):
+                bank = ps_x.tile([P, 2, 2 * P], F32, tag="x", name="bank")
+                for w in range(2):
+                    for r in range(2):
+                        nc.tensor.transpose(
+                            bank[:, w, r * P : (r + 1) * P],
+                            words[:, 2 * half + r, w * P : (w + 1) * P],
+                            ident_f32[:],
+                        )
+                copies[half](
+                    out=target_words[:, half * 2 * P : (half + 1) * 2 * P, :],
+                    in_=bank[:].rearrange("p w x -> p x w"),
+                )
+
+        def quantise(target, codes, scales):
+            nc.vector.quantize_mx(
+                out=codes[:].bitcast(FP8X4),
+                scales=scales[:],
+                in_=target[:].rearrange("p x t -> p (x t)"),
+            )
+
+        def turn_kv(b):
+            kv_grouped[b] = grouped.tile([P, N, PACK], BF16, name="kv_grouped", align_bytes=64)
+            regroup_by_transposes(kv_sb[b][:].bitcast(F32), kv_grouped[b], (nc.scalar.copy, nc.scalar.copy))
+
+        def quantise_kv(b):
+            kv_codes[b] = kv_mx.tile([P, N], U32, name="kv_codes", align_bytes=64)
+            kv_scales[b] = kv_mx.tile([P, N], U8, name="kv_scales", align_bytes=64)
+            quantise(kv_grouped[b], kv_codes[b], kv_scales[b])
+
+        def project_values(b, c, copy):
+            if c == 0:
+                v_grouped[b] = grouped.tile([P, DM, PACK], BF16, name="v_grouped", align_bytes=64)
+            cols = slice(c * P, (c + 1) * P)
+            v_ps = ps_s.tile([P, PACK, P], F32, tag="s", name="v_ps")
+            for t in range(PACK):
+                keys = slice(t * P, (t + 1) * P)
+                nc.tensor.matmul_mx(
+                    out=v_ps[:, t, :],
+                    lhsT=kv_codes[b][:, keys].bitcast(FP8X4),
+                    lhsT_scale=kv_scales[b][:, keys],
+                    rhs=w_codes[:, cols].bitcast(FP8X4),
+                    rhs_scale=w_scales[:, cols],
+                    start=True,
+                    stop=True,
+                )
+            copy(out=v_grouped[b][:, cols, :], in_=v_ps[:].rearrange("p t c -> p c t"))
+
+        def quantise_values(b):
+            v_codes[b] = v_mx.tile([P, DM], U32, name="v_codes", align_bytes=64)
+            v_scales[b] = v_mx.tile([P, DM], U8, name="v_scales", align_bytes=64)
+            quantise(v_grouped[b], v_codes[b], v_scales[b])
+
+        def turn_qk(u):
+            b, h = divmod(u, H)
+            qk_ps = ps_x.tile([P, 2, N], BF16, tag="x", name="qk_ps")
+            for a in range(TILES):
+                nc.tensor.transpose(qk_ps[:, 0, a * P : (a + 1) * P], q_sb[b][:, h, a, :], ident_bf[:])
+            for a in range(TILES):
+                nc.tensor.transpose(qk_ps[:, 1, a * P : (a + 1) * P], k_sb[b][:, h, a, :], ident_bf[:])
+            qkT[u] = turned_qk.tile([P, 2, N], BF16, name="qkT")
+            nc.scalar.copy(out=qkT[u][:], in_=qk_ps[:])
+
+        def begin_unit(u):
+            e_sb[u] = e_pool.tile([P, TILES, N], BF16, name="e_sb")
+            neg_max[u] = stats.tile([P, TILES], F32, name="neg_max")
+            row_sum[u] = stats.tile([P, TILES], F32, name="row_sum")
+
+        def scores(u, a):
+            h = u % H
+            s_ps = ps_s.tile([P, N], F32, tag="s", name="s_ps")
+            nc.tensor.matmul(
+                s_ps[:], lhsT=qkT[u][:, 0, a * P : (a + 1) * P], rhs=qkT[u][:, 1, :], start=True, stop=False
+            )
+            last_tile = a == TILES - 1
+            nc.tensor.matmul(
+                s_ps[:, a * P : (a + 1) * P],
+                lhsT=mask_same[:],
+                rhs=ident_f32[:],
+                is_transpose=True,
+                start=False,
+                stop=last_tile,
+            )
+            if not last_tile:
+                nc.tensor.matmul(
+                    s_ps[:, (a + 1) * P : (a + 2) * P],
+                    lhsT=mask_next[:],
+                    rhs=ident_f32[:],
+                    is_transpose=True,
+                    start=False,
+                    stop=True,
+                )
+            unread = scratch.tile([P, N], F32, name="unread")
+            nc.vector.tensor_scalar(
+                out=unread[:],
+                in0=s_ps[:],
+                scalar1=-SCALE,
+                scalar2=neg_sink[:, h : h + 1],
+                op0=ALU.mult,
+                op1=ALU.min,
+                accum_out=neg_max[u][:, a : a + 1],
+            )
+            nc.scalar.activation(
+                out=e_sb[u][:, a, :],
+                in_=s_ps[:],
+                func=ACT.Exp,
+                bias=neg_max[u][:, a : a + 1],
+                scale=SCALE,
+                accum_out=row_sum[u][:, a : a + 1],
+            )
+
+        def sink_term(u):
+            h = u % H
+            sink_e[u] = stats.tile([P, TILES], F32, name="sink_e")
+            nc.scalar.activation(out=sink_e[u][:], in_=neg_max[u][:], func=ACT.Exp, bias=sink_f32[:, h : h + 1], scale=1.0)
+
+        def denominators(u):
+            den = stats.tile([P, TILES], F32, name="den")
+            rden[u] = stats.tile([P, TILES], F32, name="rden")
+            nc.vector.tensor_add(out=den[:], in0=row_sum[u][:], in1=sink_e[u][:])
+            nc.vector.reciprocal(out=rden[u][:], in_=den[:])
+
+        def turn_e(u):
+            e_grouped[u] = grouped.tile([P, N, PACK], BF16, name="e_grouped", align_bytes=64)
+            regroup_by_transposes(e_sb[u][:].bitcast(F32), e_grouped[u], (nc.vector.tensor_copy, nc.scalar.copy))
+
+        def quantise_e(u):
+            e_codes[u] = e_mx.tile([P, N], U32, name="e_codes", align_bytes=64)
+            e_scales[u] = e_mx.tile([P, N], U8, name="e_scales", align_bytes=64)
+            quantise(e_grouped[u], e_codes[u], e_scales[u])
+
+        def attend(u, half, y):
+            b, h = divmod(u, H)
+            cols = slice(h * DV, (h + 1) * DV)
+            o_ps = ps_x.tile([P, 2, DV], F32, tag="x", name="o_ps")
+            for r in range(2):
+                rows = slice((2 * half + r) * P, (2 * half + r + 1) * P)
+                nc.tensor.matmul_mx(
+                    out=o_ps[:, r, :],
+                    lhsT=e_codes[u][:, rows].bitcast(FP8X4),
+                    lhsT_scale=e_scales[u][:, rows],
+                    rhs=v_codes[b][:, cols].bitcast(FP8X4),
+                    rhs_scale=v_scales[b][:, cols],
+                    start=True,
+                    stop=True,
+                )
+            for r in range(2):
+                a = 2 * half + r
+                nc.scalar.activation(out=y[:, a, :], in_=o_ps[:, r, :], func=ACT.Silu, scale=rden[u][:, a : a + 1])
+
+        load_kv(0)
+        w_raw = const.tile([P, PACK, DM], BF16, name="w_raw")
+        nc.sync.dma_start(
+            out=w_raw[:].rearrange("p (w e) c -> p w (e c)", w=2),
+            in_=Wv1.rearrange("(w p e) c -> p w (e c)", w=2, e=2),
+        )
+        load_kv(1)
+        load_qk(0)
+        load_qk(1)
+        load_kv(2)
+        sink_bf = const.tile([P, H], BF16, name="sink_bf")
+        nc.scalar.dma_start(out=sink_bf[:], in_=attn_sink.partition_broadcast(P))
+
+        ident_f32 = const.tile([P, P], F32, name="ident_f32")
+        make_identity(nc, ident_f32[:])
+        ident_bf = const.tile([P, P], BF16, name="ident_bf")
+        make_identity(nc, ident_bf[:])
+        mask_same = const.tile([P, P], F32, name="mask_same")
+        nc.gpsimd.memset(mask_same[:], 0.0)
+        nc.gpsimd.affine_select(
+            out=mask_same[:], in_=mask_same[:], compare_op=ALU.is_ge, fill=NEG,
+            base=0, pattern=[[1, P]], channel_multiplier=-1,
+        )
+        mask_next = const.tile([P, P], F32, name="mask_next")
+        nc.gpsimd.memset(mask_next[:], 0.0)
+        nc.gpsimd.affine_select(
+            out=mask_next[:], in_=mask_next[:], compare_op=ALU.is_ge, fill=NEG,
+            base=-1, pattern=[[-1, P]], channel_multiplier=1,
+        )
+
+        w_grouped = const.tile([P, DM, PACK], BF16, name="w_grouped", align_bytes=64)
+        w_codes = const.tile([P, DM], U32, name="w_codes", align_bytes=64)
+        w_scales = const.tile([P, DM], U8, name="w_scales", align_bytes=64)
+        turn_kv(0)
+        turn_kv(1)
+        nc.vector.tensor_copy(out=w_grouped[:], in_=w_raw[:].rearrange("p t c -> p c t"))
+        quantise_kv(0)
+        quantise(w_grouped, w_codes, w_scales)
+        quantise_kv(1)
+        sink_f32 = const.tile([P, H], F32, name="sink_f32")
+        neg_sink = const.tile([P, H], F32, name="neg_sink")
+        nc.vector.tensor_copy(out=sink_f32[:], in_=sink_bf[:])
+        nc.vector.tensor_scalar_mul(out=neg_sink[:], in0=sink_f32[:], scalar1=-1.0)
+        turn_qk(0)
+
+        for b in range(GROUP_BATCHES):
+            for c in range(CHUNKS):
+                project_values(b, c, nc.scalar.copy if c % 2 else nc.vector.tensor_copy)
+            quantise_values(b)
+
+        for first in range(0, UNITS, GROUP):
+            units = range(first, first + GROUP)
+            for u in units:
+                b, h = divmod(u, H)
+                if h == 0 and b + 2 < B:
+                    load_qk(b + 2)
+                if h == 0 and b + 3 < B:
+                    load_kv(b + 3)
+                if u + 1 < UNITS:
+                    turn_qk(u + 1)
+                begin_unit(u)
+                scores(u, 0)
+                scores(u, 1)
+                if u - 2 >= first:
+                    quantise_e(u - 2)
+                scores(u, 2)
+                scores(u, 3)
+                sink_term(u)
+                if u - 1 >= first:
+                    turn_e(u - 1)
+                    denominators(u - 1)
+                if h == 0 and b + GROUP_BATCHES < B:
+                    turn_kv(b + GROUP_BATCHES)
+                if h == 1 and b + GROUP_BATCHES < B:
+                    quantise_kv(b + GROUP_BATCHES)
+
+            last = first + GROUP - 1
+            next_batch = (first + GROUP) // H
+            turn_e(last)
+            quantise_e(last - 1)
+            for n, u in enumerate(units):
+                b, h = divmod(u, H)
+                y = results.tile([P, TILES, DV], F32, name="y")
+                for half in range(2):
+                    attend(u, half, y)
+                    if next_batch < B:
+                        chunk = 2 * n + half
+                        project_values(next_batch + chunk // CHUNKS, chunk % CHUNKS, nc.vector.tensor_copy)
+                        if chunk % CHUNKS == CHUNKS - 1:
+                            quantise_values(next_batch + chunk // CHUNKS)
+                nc.sync.dma_start(out=out[b, h].rearrange("(a p) c -> p a c", p=P), in_=y[:])
+                if n == 0:
+                    quantise_e(last)
+                    denominators(last)

@@ -44,7 +44,7 @@ def tile_attention_pa_t_kernel(tc, q, k1, key_values_input, Wv1, attn_sink, out)
         e_mx = stack.enter_context(tc.tile_pool(name="e_mx", bufs=GROUP + 2))
         kv_mx = stack.enter_context(tc.tile_pool(name="kv_mx", bufs=GROUP_BATCHES))
         v_mx = stack.enter_context(tc.tile_pool(name="v_mx", bufs=2 * GROUP_BATCHES))
-        results = stack.enter_context(tc.tile_pool(name="results", bufs=3))
+        results = stack.enter_context(tc.tile_pool(name="results", bufs=GROUP))
         ps_s = stack.enter_context(tc.psum_pool(name="ps_s", bufs=4))
         ps_x = stack.enter_context(tc.psum_pool(name="ps_x", bufs=4))
 
@@ -52,7 +52,7 @@ def tile_attention_pa_t_kernel(tc, q, k1, key_values_input, Wv1, attn_sink, out)
         kv_grouped, kv_codes, kv_scales = {}, {}, {}
         v_grouped, v_codes, v_scales = {}, {}, {}
         qkT, e_sb, e_grouped, e_codes, e_scales = {}, {}, {}, {}, {}
-        neg_max, row_sum, sink_e, rden = {}, {}, {}, {}
+        neg_max, row_sum, den, rden = {}, {}, {}, {}
 
         def load_qk(b):
             q_sb[b] = qk_in.tile([P, H, TILES, DH], BF16, name="q_sb")
@@ -180,16 +180,18 @@ def tile_attention_pa_t_kernel(tc, q, k1, key_values_input, Wv1, attn_sink, out)
                 accum_out=row_sum[u][:, a : a + 1],
             )
 
-        def sink_term(u):
-            h = u % H
-            sink_e[u] = stats.tile([P, TILES], F32, name="sink_e")
-            nc.scalar.activation(out=sink_e[u][:], in_=neg_max[u][:], func=ACT.Exp, bias=sink_f32[:, h : h + 1], scale=1.0)
-
         def denominators(u):
-            den = stats.tile([P, TILES], F32, name="den")
+            h = u % H
+            sink_e = stats.tile([P, TILES], F32, name="sink_e")
+            den[u] = stats.tile([P, TILES], F32, name="den")
+            nc.scalar.activation(
+                out=sink_e[:], in_=neg_max[u][:], func=ACT.Exp, bias=sink_f32[:, h : h + 1], scale=1.0
+            )
+            nc.gpsimd.tensor_add(out=den[u][:], in0=row_sum[u][:], in1=sink_e[:])
+
+        def reciprocals(u):
             rden[u] = stats.tile([P, TILES], F32, name="rden")
-            nc.vector.tensor_add(out=den[:], in0=row_sum[u][:], in1=sink_e[u][:])
-            nc.vector.reciprocal(out=rden[u][:], in_=den[:])
+            nc.vector.reciprocal(out=rden[u][:], in_=den[u][:])
 
         def turn_e(u):
             e_grouped[u] = grouped.tile([P, N, PACK], BF16, name="e_grouped", align_bytes=64)
@@ -286,10 +288,10 @@ def tile_attention_pa_t_kernel(tc, q, k1, key_values_input, Wv1, attn_sink, out)
                     quantise_e(u - 2)
                 scores(u, 2)
                 scores(u, 3)
-                sink_term(u)
+                denominators(u)
                 if u - 1 >= first:
                     turn_e(u - 1)
-                    denominators(u - 1)
+                    reciprocals(u - 1)
                 if h == 0 and b + GROUP_BATCHES < B:
                     turn_kv(b + GROUP_BATCHES)
                 if h == 1 and b + GROUP_BATCHES < B:
@@ -312,4 +314,4 @@ def tile_attention_pa_t_kernel(tc, q, k1, key_values_input, Wv1, attn_sink, out)
                 nc.sync.dma_start(out=out[b, h].rearrange("(a p) c -> p a c", p=P), in_=y[:])
                 if n == 0:
                     quantise_e(last)
-                    denominators(last)
+                    reciprocals(last)

@@ -22,6 +22,9 @@ CHUNKS = DM // P
 UNITS = B * H
 GROUP_BATCHES = 2
 GROUP = GROUP_BATCHES * H
+GROUPS = UNITS // GROUP
+LEAD_STEPS = 2
+LEAD = 2 * (GROUP - LEAD_STEPS)
 SCALE = DH**-0.5
 NEG = -3.4028234663852886e38
 
@@ -34,7 +37,7 @@ def tile_attention_pa_t_kernel(tc, q, k1, key_values_input, Wv1, attn_sink, out)
         stack.enter_context(tc.manual_schedule())
 
         const = stack.enter_context(tc.tile_pool(name="const", bufs=1))
-        qk_in = stack.enter_context(tc.tile_pool(name="qk_in", bufs=3))
+        qk_in = stack.enter_context(tc.tile_pool(name="qk_in", bufs=6))
         kv_in = stack.enter_context(tc.tile_pool(name="kv_in", bufs=3))
         turned_qk = stack.enter_context(tc.tile_pool(name="turned_qk", bufs=2))
         e_pool = stack.enter_context(tc.tile_pool(name="e_pool", bufs=3))
@@ -42,23 +45,25 @@ def tile_attention_pa_t_kernel(tc, q, k1, key_values_input, Wv1, attn_sink, out)
         stats = stack.enter_context(tc.tile_pool(name="stats", bufs=GROUP + 4))
         grouped = stack.enter_context(tc.tile_pool(name="grouped", bufs=2))
         e_mx = stack.enter_context(tc.tile_pool(name="e_mx", bufs=GROUP + 2))
-        kv_mx = stack.enter_context(tc.tile_pool(name="kv_mx", bufs=GROUP_BATCHES))
+        kv_mx = stack.enter_context(tc.tile_pool(name="kv_mx", bufs=3))
         v_mx = stack.enter_context(tc.tile_pool(name="v_mx", bufs=2 * GROUP_BATCHES))
-        results = stack.enter_context(tc.tile_pool(name="results", bufs=GROUP))
+        results = stack.enter_context(tc.tile_pool(name="results", bufs=2 * GROUP))
         ps_s = stack.enter_context(tc.psum_pool(name="ps_s", bufs=4))
         ps_x = stack.enter_context(tc.psum_pool(name="ps_x", bufs=4))
 
-        q_sb, k_sb, kv_sb = {}, {}, {}
+        q_sb, k_sb = {}, {}
+        kv_sb = {}
         kv_grouped, kv_codes, kv_scales = {}, {}, {}
         v_grouped, v_codes, v_scales = {}, {}, {}
         qkT, e_sb, e_grouped, e_codes, e_scales = {}, {}, {}, {}, {}
         neg_max, row_sum, den, rden = {}, {}, {}, {}
 
-        def load_qk(b):
-            q_sb[b] = qk_in.tile([P, H, TILES, DH], BF16, name="q_sb")
-            k_sb[b] = qk_in.tile([P, H, TILES, DH], BF16, name="k_sb")
-            nc.sync.dma_start(out=q_sb[b][:], in_=q[b].rearrange("h (a p) d -> p h a d", p=P))
-            nc.sync.dma_start(out=k_sb[b][:], in_=k1[b].rearrange("h (a p) d -> p h a d", p=P))
+        def load_qk(b, pair):
+            heads = slice(2 * pair, 2 * pair + 2)
+            q_sb[b, pair] = qk_in.tile([P, 2, TILES, DH], BF16, name="q_sb")
+            k_sb[b, pair] = qk_in.tile([P, 2, TILES, DH], BF16, name="k_sb")
+            nc.sync.dma_start(out=q_sb[b, pair][:], in_=q[b, heads].rearrange("h (a p) d -> p h a d", p=P))
+            nc.sync.dma_start(out=k_sb[b, pair][:], in_=k1[b, heads].rearrange("h (a p) d -> p h a d", p=P))
 
         def load_kv(b):
             kv_sb[b] = kv_in.tile([P, PACK, DKV], BF16, name="kv_sb")
@@ -99,7 +104,10 @@ def tile_attention_pa_t_kernel(tc, q, k1, key_values_input, Wv1, attn_sink, out)
             kv_scales[b] = kv_mx.tile([P, N], U8, name="kv_scales", align_bytes=64)
             quantise(kv_grouped[b], kv_codes[b], kv_scales[b])
 
-        def project_values(b, c, copy):
+        def project_values(chunk, copy):
+            b, c = divmod(chunk, CHUNKS)
+            if b >= B:
+                return
             if c == 0:
                 v_grouped[b] = grouped.tile([P, DM, PACK], BF16, name="v_grouped", align_bytes=64)
             cols = slice(c * P, (c + 1) * P)
@@ -116,19 +124,18 @@ def tile_attention_pa_t_kernel(tc, q, k1, key_values_input, Wv1, attn_sink, out)
                     stop=True,
                 )
             copy(out=v_grouped[b][:, cols, :], in_=v_ps[:].rearrange("p t c -> p c t"))
-
-        def quantise_values(b):
-            v_codes[b] = v_mx.tile([P, DM], U32, name="v_codes", align_bytes=64)
-            v_scales[b] = v_mx.tile([P, DM], U8, name="v_scales", align_bytes=64)
-            quantise(v_grouped[b], v_codes[b], v_scales[b])
+            if c == CHUNKS - 1:
+                v_codes[b] = v_mx.tile([P, DM], U32, name="v_codes", align_bytes=64)
+                v_scales[b] = v_mx.tile([P, DM], U8, name="v_scales", align_bytes=64)
+                quantise(v_grouped[b], v_codes[b], v_scales[b])
 
         def turn_qk(u):
             b, h = divmod(u, H)
             qk_ps = ps_x.tile([P, 2, N], BF16, tag="x", name="qk_ps")
             for a in range(TILES):
-                nc.tensor.transpose(qk_ps[:, 0, a * P : (a + 1) * P], q_sb[b][:, h, a, :], ident_bf[:])
+                nc.tensor.transpose(qk_ps[:, 0, a * P : (a + 1) * P], q_sb[b, h // 2][:, h % 2, a, :], ident_bf[:])
             for a in range(TILES):
-                nc.tensor.transpose(qk_ps[:, 1, a * P : (a + 1) * P], k_sb[b][:, h, a, :], ident_bf[:])
+                nc.tensor.transpose(qk_ps[:, 1, a * P : (a + 1) * P], k_sb[b, h // 2][:, h % 2, a, :], ident_bf[:])
             qkT[u] = turned_qk.tile([P, 2, N], BF16, name="qkT")
             nc.scalar.copy(out=qkT[u][:], in_=qk_ps[:])
 
@@ -193,16 +200,16 @@ def tile_attention_pa_t_kernel(tc, q, k1, key_values_input, Wv1, attn_sink, out)
             rden[u] = stats.tile([P, TILES], F32, name="rden")
             nc.vector.reciprocal(out=rden[u][:], in_=den[u][:])
 
-        def turn_e(u):
+        def turn_e(u, copies):
             e_grouped[u] = grouped.tile([P, N, PACK], BF16, name="e_grouped", align_bytes=64)
-            regroup_by_transposes(e_sb[u][:].bitcast(F32), e_grouped[u], (nc.vector.tensor_copy, nc.scalar.copy))
+            regroup_by_transposes(e_sb[u][:].bitcast(F32), e_grouped[u], copies)
 
         def quantise_e(u):
             e_codes[u] = e_mx.tile([P, N], U32, name="e_codes", align_bytes=64)
             e_scales[u] = e_mx.tile([P, N], U8, name="e_scales", align_bytes=64)
             quantise(e_grouped[u], e_codes[u], e_scales[u])
 
-        def attend(u, half, y):
+        def attend(u, half):
             b, h = divmod(u, H)
             cols = slice(h * DV, (h + 1) * DV)
             o_ps = ps_x.tile([P, 2, DV], F32, tag="x", name="o_ps")
@@ -217,27 +224,32 @@ def tile_attention_pa_t_kernel(tc, q, k1, key_values_input, Wv1, attn_sink, out)
                     start=True,
                     stop=True,
                 )
+            y = results.tile([P, 2, DV], F32, name="y")
             for r in range(2):
                 a = 2 * half + r
-                nc.scalar.activation(out=y[:, a, :], in_=o_ps[:, r, :], func=ACT.Silu, scale=rden[u][:, a : a + 1])
+                nc.scalar.activation(out=y[:, r, :], in_=o_ps[:, r, :], func=ACT.Silu, scale=rden[u][:, a : a + 1])
+            queries = slice(2 * half * P, (2 * half + 2) * P)
+            nc.sync.dma_start(out=out[b, h, queries, :].rearrange("(r p) c -> p r c", p=P), in_=y[:])
 
+        load_qk(0, 0)
         load_kv(0)
+        load_qk(0, 1)
         w_raw = const.tile([P, PACK, DM], BF16, name="w_raw")
         nc.sync.dma_start(
             out=w_raw[:].rearrange("p (w e) c -> p w (e c)", w=2),
             in_=Wv1.rearrange("(w p e) c -> p w (e c)", w=2, e=2),
         )
         load_kv(1)
-        load_qk(0)
-        load_qk(1)
+        load_qk(1, 0)
+        load_qk(1, 1)
         load_kv(2)
         sink_bf = const.tile([P, H], BF16, name="sink_bf")
         nc.scalar.dma_start(out=sink_bf[:], in_=attn_sink.partition_broadcast(P))
 
-        ident_f32 = const.tile([P, P], F32, name="ident_f32")
-        make_identity(nc, ident_f32[:])
         ident_bf = const.tile([P, P], BF16, name="ident_bf")
         make_identity(nc, ident_bf[:])
+        ident_f32 = const.tile([P, P], F32, name="ident_f32")
+        make_identity(nc, ident_f32[:])
         mask_same = const.tile([P, P], F32, name="mask_same")
         nc.gpsimd.memset(mask_same[:], 0.0)
         nc.gpsimd.affine_select(
@@ -250,68 +262,61 @@ def tile_attention_pa_t_kernel(tc, q, k1, key_values_input, Wv1, attn_sink, out)
             out=mask_next[:], in_=mask_next[:], compare_op=ALU.is_ge, fill=NEG,
             base=-1, pattern=[[-1, P]], channel_multiplier=1,
         )
-
-        w_grouped = const.tile([P, DM, PACK], BF16, name="w_grouped", align_bytes=64)
-        w_codes = const.tile([P, DM], U32, name="w_codes", align_bytes=64)
-        w_scales = const.tile([P, DM], U8, name="w_scales", align_bytes=64)
-        turn_kv(0)
-        turn_kv(1)
-        nc.vector.tensor_copy(out=w_grouped[:], in_=w_raw[:].rearrange("p t c -> p c t"))
-        quantise_kv(0)
-        quantise(w_grouped, w_codes, w_scales)
-        quantise_kv(1)
         sink_f32 = const.tile([P, H], F32, name="sink_f32")
         neg_sink = const.tile([P, H], F32, name="neg_sink")
         nc.vector.tensor_copy(out=sink_f32[:], in_=sink_bf[:])
         nc.vector.tensor_scalar_mul(out=neg_sink[:], in0=sink_f32[:], scalar1=-1.0)
+        w_grouped = const.tile([P, DM, PACK], BF16, name="w_grouped", align_bytes=64)
+        w_codes = const.tile([P, DM], U32, name="w_codes", align_bytes=64)
+        w_scales = const.tile([P, DM], U8, name="w_scales", align_bytes=64)
         turn_qk(0)
 
-        for b in range(GROUP_BATCHES):
-            for c in range(CHUNKS):
-                project_values(b, c, nc.scalar.copy if c % 2 else nc.vector.tensor_copy)
-            quantise_values(b)
-
-        for first in range(0, UNITS, GROUP):
-            units = range(first, first + GROUP)
-            for u in units:
+        one_each = (nc.vector.tensor_copy, nc.scalar.copy)
+        both_vector = (nc.vector.tensor_copy, nc.vector.tensor_copy)
+        for g in range(GROUPS):
+            first = g * GROUP
+            kv_first = 0 if g == 0 else GROUP_BATCHES * (g + 1)
+            kv_end = min(B, GROUP_BATCHES * (g + 2))
+            for n in range(GROUP):
+                u = first + n
                 b, h = divmod(u, H)
                 if h == 0 and b + 2 < B:
-                    load_qk(b + 2)
-                if h == 0 and b + 3 < B:
-                    load_kv(b + 3)
+                    load_qk(b + 2, 0)
+                    load_qk(b + 2, 1)
                 if u + 1 < UNITS:
                     turn_qk(u + 1)
                 begin_unit(u)
                 scores(u, 0)
                 scores(u, 1)
-                if u - 2 >= first:
+                if n >= 2:
                     quantise_e(u - 2)
                 scores(u, 2)
                 scores(u, 3)
                 denominators(u)
-                if u - 1 >= first:
-                    turn_e(u - 1)
+                if n >= 1:
+                    turn_e(u - 1, one_each)
                     reciprocals(u - 1)
-                if h == 0 and b + GROUP_BATCHES < B:
-                    turn_kv(b + GROUP_BATCHES)
-                if h == 1 and b + GROUP_BATCHES < B:
-                    quantise_kv(b + GROUP_BATCHES)
+                if g == 0 and n == LEAD_STEPS - 1:
+                    nc.vector.tensor_copy(out=w_grouped[:], in_=w_raw[:].rearrange("p t c -> p c t"))
+                    quantise(w_grouped, w_codes, w_scales)
+                kv_b = kv_first + n // 2
+                if kv_b < kv_end and n % 2 == 0:
+                    turn_kv(kv_b)
+                    if kv_b + 3 < B:
+                        load_kv(kv_b + 3)
+                if kv_b < kv_end and n % 2 == 1:
+                    quantise_kv(kv_b)
+                if g == 0 and n >= LEAD_STEPS:
+                    project_values(2 * (n - LEAD_STEPS), nc.vector.tensor_copy)
+                    project_values(2 * (n - LEAD_STEPS) + 1, nc.scalar.copy)
 
             last = first + GROUP - 1
-            next_batch = (first + GROUP) // H
-            turn_e(last)
+            turn_e(last, both_vector)
             quantise_e(last - 1)
-            for n, u in enumerate(units):
-                b, h = divmod(u, H)
-                y = results.tile([P, TILES, DV], F32, name="y")
+            for n in range(GROUP):
                 for half in range(2):
-                    attend(u, half, y)
-                    if next_batch < B:
-                        chunk = 2 * n + half
-                        project_values(next_batch + chunk // CHUNKS, chunk % CHUNKS, nc.vector.tensor_copy)
-                        if chunk % CHUNKS == CHUNKS - 1:
-                            quantise_values(next_batch + chunk // CHUNKS)
-                nc.sync.dma_start(out=out[b, h].rearrange("(a p) c -> p a c", p=P), in_=y[:])
+                    attend(first + n, half)
+                    project_values(LEAD + 2 * GROUP * g + 2 * n + half, nc.vector.tensor_copy)
                 if n == 0:
                     quantise_e(last)
                     reciprocals(last)

@@ -97,7 +97,7 @@ def tile_attention_pa_t_kernel(tc, q, k1, key_values_input, Wv1, attn_sink, out)
 
         def turn_kv(b):
             kv_grouped[b] = grouped.tile([P, N, PACK], BF16, name="kv_grouped", align_bytes=64)
-            regroup_by_transposes(kv_sb[b][:].bitcast(F32), kv_grouped[b], (nc.scalar.copy, nc.scalar.copy))
+            regroup_by_transposes(kv_sb[b][:].bitcast(F32), kv_grouped[b], (nc.vector.tensor_copy, nc.scalar.copy))
 
         def quantise_kv(b):
             kv_codes[b] = kv_mx.tile([P, N], U32, name="kv_codes", align_bytes=64)
@@ -262,6 +262,10 @@ def tile_attention_pa_t_kernel(tc, q, k1, key_values_input, Wv1, attn_sink, out)
             out=mask_next[:], in_=mask_next[:], compare_op=ALU.is_ge, fill=NEG,
             base=-1, pattern=[[-1, P]], channel_multiplier=1,
         )
+        zero = const.tile([P, 1], F32, name="zero")
+        one = const.tile([P, 1], F32, name="one")
+        nc.vector.memset(zero[:], 0.0)
+        nc.scalar.activation(out=one[:], in_=zero[:], func=ACT.Exp)
         sink_f32 = const.tile([P, H], F32, name="sink_f32")
         neg_sink = const.tile([P, H], F32, name="neg_sink")
         nc.vector.tensor_copy(out=sink_f32[:], in_=sink_bf[:])
@@ -286,16 +290,14 @@ def tile_attention_pa_t_kernel(tc, q, k1, key_values_input, Wv1, attn_sink, out)
                 if u + 1 < UNITS:
                     turn_qk(u + 1)
                 begin_unit(u)
-                scores(u, 0)
-                scores(u, 1)
-                if n >= 2:
-                    quantise_e(u - 2)
-                scores(u, 2)
-                scores(u, 3)
+                for a in range(TILES):
+                    scores(u, a)
                 denominators(u)
                 if n >= 1:
                     turn_e(u - 1, one_each)
                     reciprocals(u - 1)
+                if n >= 2:
+                    quantise_e(u - 2)
                 if g == 0 and n == LEAD_STEPS - 1:
                     nc.vector.tensor_copy(out=w_grouped[:], in_=w_raw[:].rearrange("p t c -> p c t"))
                     quantise(w_grouped, w_codes, w_scales)

@@ -20,11 +20,13 @@ PACK = 4
 TILES = N // P
 CHUNKS = DM // P
 UNITS = B * H
-GROUP_BATCHES = 2
+GROUP_BATCHES = 4
 GROUP = GROUP_BATCHES * H
 GROUPS = UNITS // GROUP
 LEAD_STEPS = 2
-LEAD = 2 * (GROUP - LEAD_STEPS)
+LEAD = 12
+KV_STEPS = 2
+KV_FIRST = 6
 SCALE = DH**-0.5
 NEG = -3.4028234663852886e38
 
@@ -41,13 +43,13 @@ def tile_attention_pa_t_kernel(tc, q, k1, key_values_input, Wv1, attn_sink, out)
         kv_in = stack.enter_context(tc.tile_pool(name="kv_in", bufs=3))
         turned_qk = stack.enter_context(tc.tile_pool(name="turned_qk", bufs=2))
         e_pool = stack.enter_context(tc.tile_pool(name="e_pool", bufs=3))
-        scratch = stack.enter_context(tc.tile_pool(name="scratch", bufs=4))
+        scratch = stack.enter_context(tc.tile_pool(name="scratch", bufs=2))
         stats = stack.enter_context(tc.tile_pool(name="stats", bufs=GROUP + 4))
         grouped = stack.enter_context(tc.tile_pool(name="grouped", bufs=2))
         e_mx = stack.enter_context(tc.tile_pool(name="e_mx", bufs=GROUP + 2))
-        kv_mx = stack.enter_context(tc.tile_pool(name="kv_mx", bufs=3))
-        v_mx = stack.enter_context(tc.tile_pool(name="v_mx", bufs=2 * GROUP_BATCHES))
-        results = stack.enter_context(tc.tile_pool(name="results", bufs=2 * GROUP))
+        kv_mx = stack.enter_context(tc.tile_pool(name="kv_mx", bufs=KV_FIRST))
+        v_mx = stack.enter_context(tc.tile_pool(name="v_mx", bufs=4))
+        results = stack.enter_context(tc.tile_pool(name="results", bufs=GROUP))
         ps_s = stack.enter_context(tc.psum_pool(name="ps_s", bufs=4))
         ps_x = stack.enter_context(tc.psum_pool(name="ps_x", bufs=4))
 
@@ -270,7 +272,7 @@ def tile_attention_pa_t_kernel(tc, q, k1, key_values_input, Wv1, attn_sink, out)
         neg_sink = const.tile([P, H], F32, name="neg_sink")
         nc.vector.tensor_copy(out=sink_f32[:], in_=sink_bf[:])
         nc.vector.tensor_scalar_mul(out=neg_sink[:], in0=sink_f32[:], scalar1=-1.0)
-        w_grouped = const.tile([P, DM, PACK], BF16, name="w_grouped", align_bytes=64)
+        w_grouped = grouped.tile([P, DM, PACK], BF16, tag="v_grouped", name="w_grouped", align_bytes=64)
         w_codes = const.tile([P, DM], U32, name="w_codes", align_bytes=64)
         w_scales = const.tile([P, DM], U8, name="w_scales", align_bytes=64)
         turn_qk(0)
@@ -279,8 +281,7 @@ def tile_attention_pa_t_kernel(tc, q, k1, key_values_input, Wv1, attn_sink, out)
         both_vector = (nc.vector.tensor_copy, nc.vector.tensor_copy)
         for g in range(GROUPS):
             first = g * GROUP
-            kv_first = 0 if g == 0 else GROUP_BATCHES * (g + 1)
-            kv_end = min(B, GROUP_BATCHES * (g + 2))
+            kv_first, kv_end = (0, KV_FIRST) if g == 0 else (KV_FIRST, B)
             for n in range(GROUP):
                 u = first + n
                 b, h = divmod(u, H)
@@ -301,14 +302,14 @@ def tile_attention_pa_t_kernel(tc, q, k1, key_values_input, Wv1, attn_sink, out)
                 if g == 0 and n == LEAD_STEPS - 1:
                     nc.vector.tensor_copy(out=w_grouped[:], in_=w_raw[:].rearrange("p t c -> p c t"))
                     quantise(w_grouped, w_codes, w_scales)
-                kv_b = kv_first + n // 2
-                if kv_b < kv_end and n % 2 == 0:
+                kv_b = kv_first + n // KV_STEPS
+                if kv_b < kv_end and n % KV_STEPS == 0:
                     turn_kv(kv_b)
                     if kv_b + 3 < B:
                         load_kv(kv_b + 3)
-                if kv_b < kv_end and n % 2 == 1:
+                if kv_b < kv_end and n % KV_STEPS == 1:
                     quantise_kv(kv_b)
-                if g == 0 and n >= LEAD_STEPS:
+                if g == 0 and 0 <= n - LEAD_STEPS < LEAD // 2:
                     project_values(2 * (n - LEAD_STEPS), nc.vector.tensor_copy)
                     project_values(2 * (n - LEAD_STEPS) + 1, nc.scalar.copy)
 

@@ -10,6 +10,7 @@ U8 = mybir.dt.uint8
 FP8X4 = mybir.dt.float8_e4m3fn_x4
 ACT = mybir.ActivationFunctionType
 ALU = mybir.AluOpType
+AXIS = mybir.AxisListType
 
 B, H, N, DH = 8, 4, 512, 128
 DV = 256
@@ -43,7 +44,6 @@ def tile_attention_pa_t_kernel(tc, q, k1, key_values_input, Wv1, attn_sink, out)
         kv_in = stack.enter_context(tc.tile_pool(name="kv_in", bufs=3))
         turned_qk = stack.enter_context(tc.tile_pool(name="turned_qk", bufs=2))
         e_pool = stack.enter_context(tc.tile_pool(name="e_pool", bufs=3))
-        scratch = stack.enter_context(tc.tile_pool(name="scratch", bufs=2))
         stats = stack.enter_context(tc.tile_pool(name="stats", bufs=GROUP + 4))
         grouped = stack.enter_context(tc.tile_pool(name="grouped", bufs=2))
         e_mx = stack.enter_context(tc.tile_pool(name="e_mx", bufs=GROUP + 2))
@@ -58,7 +58,7 @@ def tile_attention_pa_t_kernel(tc, q, k1, key_values_input, Wv1, attn_sink, out)
         kv_grouped, kv_codes, kv_scales = {}, {}, {}
         v_grouped, v_codes, v_scales = {}, {}, {}
         qkT, e_sb, e_grouped, e_codes, e_scales = {}, {}, {}, {}, {}
-        neg_max, row_sum, den, rden = {}, {}, {}, {}
+        row_max, neg_max, row_sum, den, rden = {}, {}, {}, {}, {}
 
         def load_qk(b, pair):
             heads = slice(2 * pair, 2 * pair + 2)
@@ -143,6 +143,7 @@ def tile_attention_pa_t_kernel(tc, q, k1, key_values_input, Wv1, attn_sink, out)
 
         def begin_unit(u):
             e_sb[u] = e_pool.tile([P, TILES, N], BF16, name="e_sb")
+            row_max[u] = stats.tile([P, TILES], F32, name="row_max")
             neg_max[u] = stats.tile([P, TILES], F32, name="neg_max")
             row_sum[u] = stats.tile([P, TILES], F32, name="row_sum")
 
@@ -170,15 +171,14 @@ def tile_attention_pa_t_kernel(tc, q, k1, key_values_input, Wv1, attn_sink, out)
                     start=False,
                     stop=True,
                 )
-            unread = scratch.tile([P, N], F32, name="unread")
-            nc.vector.tensor_scalar(
-                out=unread[:],
-                in0=s_ps[:],
+            nc.vector.tensor_reduce(out=row_max[u][:, a : a + 1], in_=s_ps[:], op=ALU.max, axis=AXIS.X)
+            nc.gpsimd.tensor_scalar(
+                out=neg_max[u][:, a : a + 1],
+                in0=row_max[u][:, a : a + 1],
                 scalar1=-SCALE,
                 scalar2=neg_sink[:, h : h + 1],
                 op0=ALU.mult,
                 op1=ALU.min,
-                accum_out=neg_max[u][:, a : a + 1],
             )
             nc.scalar.activation(
                 out=e_sb[u][:, a, :],

@@ -19,15 +19,15 @@ DM = H * DV
 P = 128
 PACK = 4
 TILES = N // P
-CHUNKS = DM // P
+CHUNKS = DV // P
 UNITS = B * H
-GROUP_BATCHES = 4
-GROUP = GROUP_BATCHES * H
-GROUPS = UNITS // GROUP
-LEAD_STEPS = 2
-LEAD = 12
-KV_STEPS = 2
-KV_FIRST = 6
+W_HALVES = DM // N
+W_PIECES = 2
+W_STEP = 2
+KV_STEP = 7
+KV_EVERY = 3
+LEAD = 6
+LEAD_STEP = 29
 SCALE = DH**-0.5
 NEG = -3.4028234663852886e38
 
@@ -40,39 +40,55 @@ def tile_attention_pa_t_kernel(tc, q, k1, key_values_input, Wv1, attn_sink, out)
         stack.enter_context(tc.manual_schedule())
 
         const = stack.enter_context(tc.tile_pool(name="const", bufs=1))
-        qk_in = stack.enter_context(tc.tile_pool(name="qk_in", bufs=6))
+        qk_in = stack.enter_context(tc.tile_pool(name="qk_in", bufs=4))
         kv_in = stack.enter_context(tc.tile_pool(name="kv_in", bufs=3))
-        turned_qk = stack.enter_context(tc.tile_pool(name="turned_qk", bufs=2))
+        turned_qk = stack.enter_context(tc.tile_pool(name="turned_qk", bufs=3))
         e_pool = stack.enter_context(tc.tile_pool(name="e_pool", bufs=3))
-        stats = stack.enter_context(tc.tile_pool(name="stats", bufs=GROUP + 4))
+        stats = stack.enter_context(tc.tile_pool(name="stats", bufs=3))
         grouped = stack.enter_context(tc.tile_pool(name="grouped", bufs=2))
-        e_mx = stack.enter_context(tc.tile_pool(name="e_mx", bufs=GROUP + 2))
-        kv_mx = stack.enter_context(tc.tile_pool(name="kv_mx", bufs=KV_FIRST))
-        v_mx = stack.enter_context(tc.tile_pool(name="v_mx", bufs=4))
-        results = stack.enter_context(tc.tile_pool(name="results", bufs=GROUP))
+        e_mx = stack.enter_context(tc.tile_pool(name="e_mx", bufs=UNITS))
+        kept_stats = stack.enter_context(tc.tile_pool(name="kept_stats", bufs=B))
+        kv_mx = stack.enter_context(tc.tile_pool(name="kv_mx", bufs=B))
+        v_mx = stack.enter_context(tc.tile_pool(name="v_mx", bufs=LEAD // CHUNKS + 2))
+        results = stack.enter_context(tc.tile_pool(name="results", bufs=12))
         ps_s = stack.enter_context(tc.psum_pool(name="ps_s", bufs=4))
         ps_x = stack.enter_context(tc.psum_pool(name="ps_x", bufs=4))
 
         q_sb, k_sb = {}, {}
-        kv_sb = {}
+        raw = {}
         kv_grouped, kv_codes, kv_scales = {}, {}, {}
+        w_grouped = {}
         v_grouped, v_codes, v_scales = {}, {}, {}
         qkT, e_sb, e_grouped, e_codes, e_scales = {}, {}, {}, {}, {}
+        s_banks = {}
         row_max, neg_max, row_sum, den, rden = {}, {}, {}, {}, {}
 
-        def load_qk(b, pair):
-            heads = slice(2 * pair, 2 * pair + 2)
+        def load_qk(b, pair, by_head=False):
             q_sb[b, pair] = qk_in.tile([P, 2, TILES, DH], BF16, name="q_sb")
             k_sb[b, pair] = qk_in.tile([P, 2, TILES, DH], BF16, name="k_sb")
-            nc.sync.dma_start(out=q_sb[b, pair][:], in_=q[b, heads].rearrange("h (a p) d -> p h a d", p=P))
-            nc.sync.dma_start(out=k_sb[b, pair][:], in_=k1[b, heads].rearrange("h (a p) d -> p h a d", p=P))
+            step = 1 if by_head else 2
+            for j in range(0, 2, step):
+                heads = slice(2 * pair + j, 2 * pair + j + step)
+                for source, target in ((q, q_sb), (k1, k_sb)):
+                    nc.sync.dma_start(
+                        out=target[b, pair][:, j : j + step],
+                        in_=source[b, heads].rearrange("h (a p) d -> p h a d", p=P),
+                    )
 
         def load_kv(b):
-            kv_sb[b] = kv_in.tile([P, PACK, DKV], BF16, name="kv_sb")
+            raw[b] = kv_in.tile([P, PACK, DKV], BF16, name="raw")
             nc.sync.dma_start(
-                out=kv_sb[b][:].rearrange("p (w e) f -> p w (e f)", w=2),
+                out=raw[b][:].rearrange("p (w e) f -> p w (e f)", w=2),
                 in_=key_values_input[b].rearrange("(w p e) f -> p w (e f)", w=2, e=2),
             )
+
+        def load_w(half):
+            raw["w", half] = kv_in.tile([P, PACK, N], BF16, name="raw")
+            for w in range(2):
+                nc.sync.dma_start(
+                    out=raw["w", half][:, 2 * w : 2 * w + 2, :],
+                    in_=Wv1[256 * w : 256 * (w + 1), half * N : (half + 1) * N].rearrange("(p e) c -> p e c", e=2),
+                )
 
         def regroup_by_transposes(words, target, copies):
             target_words = target[:].bitcast(F32)
@@ -92,27 +108,45 @@ def tile_attention_pa_t_kernel(tc, q, k1, key_values_input, Wv1, attn_sink, out)
 
         def quantise(target, codes, scales):
             nc.vector.quantize_mx(
-                out=codes[:].bitcast(FP8X4),
-                scales=scales[:],
+                out=codes.bitcast(FP8X4),
+                scales=scales,
                 in_=target[:].rearrange("p x t -> p (x t)"),
             )
 
+        def group_w(half, piece):
+            if piece == 0:
+                w_grouped[half] = grouped.tile([P, N, PACK], BF16, tag="kv_grouped", name="w_grouped", align_bytes=64)
+            cols = slice(piece * P, (piece + 1) * P)
+            nc.gpsimd.tensor_scalar(
+                out=w_grouped[half][:, cols, :],
+                in0=raw["w", half][:, :, cols].rearrange("p t c -> p c t"),
+                scalar1=1.0,
+                scalar2=0.0,
+                op0=ALU.mult,
+                op1=ALU.add,
+            )
+
+        def quantise_w(half):
+            cols = slice(half * N, (half + 1) * N)
+            quantise(w_grouped[half], w_codes[:, cols], w_scales[:, cols])
+
         def turn_kv(b):
-            kv_grouped[b] = grouped.tile([P, N, PACK], BF16, name="kv_grouped", align_bytes=64)
-            regroup_by_transposes(kv_sb[b][:].bitcast(F32), kv_grouped[b], (nc.vector.tensor_copy, nc.scalar.copy))
+            kv_grouped[b] = grouped.tile([P, N, PACK], BF16, tag="kv_grouped", name="kv_grouped", align_bytes=64)
+            regroup_by_transposes(raw[b][:].bitcast(F32), kv_grouped[b], one_each)
 
         def quantise_kv(b):
             kv_codes[b] = kv_mx.tile([P, N], U32, name="kv_codes", align_bytes=64)
             kv_scales[b] = kv_mx.tile([P, N], U8, name="kv_scales", align_bytes=64)
-            quantise(kv_grouped[b], kv_codes[b], kv_scales[b])
+            quantise(kv_grouped[b], kv_codes[b][:], kv_scales[b][:])
 
         def project_values(chunk, copy):
-            b, c = divmod(chunk, CHUNKS)
-            if b >= B:
+            u, c = divmod(chunk, CHUNKS)
+            if u >= UNITS:
                 return
+            b, h = divmod(u, H)
             if c == 0:
-                v_grouped[b] = grouped.tile([P, DM, PACK], BF16, name="v_grouped", align_bytes=64)
-            cols = slice(c * P, (c + 1) * P)
+                v_grouped[u] = grouped.tile([P, DV, PACK], BF16, name="v_grouped", align_bytes=64)
+            cols = slice(h * DV + c * P, h * DV + (c + 1) * P)
             v_ps = ps_s.tile([P, PACK, P], F32, tag="s", name="v_ps")
             for t in range(PACK):
                 keys = slice(t * P, (t + 1) * P)
@@ -125,11 +159,14 @@ def tile_attention_pa_t_kernel(tc, q, k1, key_values_input, Wv1, attn_sink, out)
                     start=True,
                     stop=True,
                 )
-            copy(out=v_grouped[b][:, cols, :], in_=v_ps[:].rearrange("p t c -> p c t"))
-            if c == CHUNKS - 1:
-                v_codes[b] = v_mx.tile([P, DM], U32, name="v_codes", align_bytes=64)
-                v_scales[b] = v_mx.tile([P, DM], U8, name="v_scales", align_bytes=64)
-                quantise(v_grouped[b], v_codes[b], v_scales[b])
+            copy(out=v_grouped[u][:, c * P : (c + 1) * P, :], in_=v_ps[:].rearrange("p t c -> p c t"))
+
+        def quantise_v(u):
+            if u >= UNITS:
+                return
+            v_codes[u] = v_mx.tile([P, DV], U32, name="v_codes", align_bytes=64)
+            v_scales[u] = v_mx.tile([P, DV], U8, name="v_scales", align_bytes=64)
+            quantise(v_grouped[u], v_codes[u][:], v_scales[u][:])
 
         def turn_qk(u):
             b, h = divmod(u, H)
@@ -142,14 +179,17 @@ def tile_attention_pa_t_kernel(tc, q, k1, key_values_input, Wv1, attn_sink, out)
             nc.scalar.copy(out=qkT[u][:], in_=qk_ps[:])
 
         def begin_unit(u):
+            b, h = divmod(u, H)
             e_sb[u] = e_pool.tile([P, TILES, N], BF16, name="e_sb")
-            row_max[u] = stats.tile([P, TILES], F32, name="row_max")
-            neg_max[u] = stats.tile([P, TILES], F32, name="neg_max")
-            row_sum[u] = stats.tile([P, TILES], F32, name="row_sum")
+            if h == 0:
+                row_max[b] = stats.tile([P, H, TILES], F32, name="row_max")
+                neg_max[b] = stats.tile([P, H, TILES], F32, name="neg_max")
+                row_sum[b] = stats.tile([P, H, TILES], F32, name="row_sum")
 
         def scores(u, a):
-            h = u % H
+            b, h = divmod(u, H)
             s_ps = ps_s.tile([P, N], F32, tag="s", name="s_ps")
+            s_banks[u, a] = s_ps
             nc.tensor.matmul(
                 s_ps[:], lhsT=qkT[u][:, 0, a * P : (a + 1) * P], rhs=qkT[u][:, 1, :], start=True, stop=False
             )
@@ -171,36 +211,39 @@ def tile_attention_pa_t_kernel(tc, q, k1, key_values_input, Wv1, attn_sink, out)
                     start=False,
                     stop=True,
                 )
-            nc.vector.tensor_reduce(out=row_max[u][:, a : a + 1], in_=s_ps[:], op=ALU.max, axis=AXIS.X)
+            nc.vector.tensor_reduce(out=row_max[b][:, h, a : a + 1], in_=s_ps[:], op=ALU.max, axis=AXIS.X)
             nc.gpsimd.tensor_scalar(
-                out=neg_max[u][:, a : a + 1],
-                in0=row_max[u][:, a : a + 1],
+                out=neg_max[b][:, h, a : a + 1],
+                in0=row_max[b][:, h, a : a + 1],
                 scalar1=-SCALE,
                 scalar2=neg_sink[:, h : h + 1],
                 op0=ALU.mult,
                 op1=ALU.min,
             )
+
+        def exponentials(u, a):
+            b, h = divmod(u, H)
             nc.scalar.activation(
                 out=e_sb[u][:, a, :],
-                in_=s_ps[:],
+                in_=s_banks[u, a][:],
                 func=ACT.Exp,
-                bias=neg_max[u][:, a : a + 1],
+                bias=neg_max[b][:, h, a : a + 1],
                 scale=SCALE,
-                accum_out=row_sum[u][:, a : a + 1],
+                accum_out=row_sum[b][:, h, a : a + 1],
             )
 
-        def denominators(u):
-            h = u % H
-            sink_e = stats.tile([P, TILES], F32, name="sink_e")
-            den[u] = stats.tile([P, TILES], F32, name="den")
-            nc.scalar.activation(
-                out=sink_e[:], in_=neg_max[u][:], func=ACT.Exp, bias=sink_f32[:, h : h + 1], scale=1.0
-            )
-            nc.gpsimd.tensor_add(out=den[u][:], in0=row_sum[u][:], in1=sink_e[:])
+        def denominators(b):
+            sink_arg = stats.tile([P, H, TILES], F32, name="sink_arg")
+            sink_e = stats.tile([P, H, TILES], F32, name="sink_e")
+            den[b] = stats.tile([P, H, TILES], F32, name="den")
+            sinks = sink_f32[:].unsqueeze(2).broadcast_to([P, H, TILES])
+            nc.gpsimd.tensor_add(out=sink_arg[:], in0=neg_max[b][:], in1=sinks)
+            nc.scalar.activation(out=sink_e[:], in_=sink_arg[:], func=ACT.Exp)
+            nc.gpsimd.tensor_add(out=den[b][:], in0=row_sum[b][:], in1=sink_e[:])
 
-        def reciprocals(u):
-            rden[u] = stats.tile([P, TILES], F32, name="rden")
-            nc.vector.reciprocal(out=rden[u][:], in_=den[u][:])
+        def reciprocals(b):
+            rden[b] = kept_stats.tile([P, H, TILES], F32, name="rden")
+            nc.vector.reciprocal(out=rden[b][:], in_=den[b][:])
 
         def turn_e(u, copies):
             e_grouped[u] = grouped.tile([P, N, PACK], BF16, name="e_grouped", align_bytes=64)
@@ -209,11 +252,10 @@ def tile_attention_pa_t_kernel(tc, q, k1, key_values_input, Wv1, attn_sink, out)
         def quantise_e(u):
             e_codes[u] = e_mx.tile([P, N], U32, name="e_codes", align_bytes=64)
             e_scales[u] = e_mx.tile([P, N], U8, name="e_scales", align_bytes=64)
-            quantise(e_grouped[u], e_codes[u], e_scales[u])
+            quantise(e_grouped[u], e_codes[u][:], e_scales[u][:])
 
         def attend(u, half):
             b, h = divmod(u, H)
-            cols = slice(h * DV, (h + 1) * DV)
             o_ps = ps_x.tile([P, 2, DV], F32, tag="x", name="o_ps")
             for r in range(2):
                 rows = slice((2 * half + r) * P, (2 * half + r + 1) * P)
@@ -221,32 +263,29 @@ def tile_attention_pa_t_kernel(tc, q, k1, key_values_input, Wv1, attn_sink, out)
                     out=o_ps[:, r, :],
                     lhsT=e_codes[u][:, rows].bitcast(FP8X4),
                     lhsT_scale=e_scales[u][:, rows],
-                    rhs=v_codes[b][:, cols].bitcast(FP8X4),
-                    rhs_scale=v_scales[b][:, cols],
+                    rhs=v_codes[u][:].bitcast(FP8X4),
+                    rhs_scale=v_scales[u][:],
                     start=True,
                     stop=True,
                 )
             y = results.tile([P, 2, DV], F32, name="y")
             for r in range(2):
                 a = 2 * half + r
-                nc.scalar.activation(out=y[:, r, :], in_=o_ps[:, r, :], func=ACT.Silu, scale=rden[u][:, a : a + 1])
+                nc.scalar.activation(
+                    out=y[:, r, :], in_=o_ps[:, r, :], func=ACT.Silu, scale=rden[b][:, h, a : a + 1]
+                )
             queries = slice(2 * half * P, (2 * half + 2) * P)
             nc.sync.dma_start(out=out[b, h, queries, :].rearrange("(r p) c -> p r c", p=P), in_=y[:])
 
-        load_qk(0, 0)
-        load_kv(0)
-        load_qk(0, 1)
-        w_raw = const.tile([P, PACK, DM], BF16, name="w_raw")
-        nc.sync.dma_start(
-            out=w_raw[:].rearrange("p (w e) c -> p w (e c)", w=2),
-            in_=Wv1.rearrange("(w p e) c -> p w (e c)", w=2, e=2),
-        )
-        load_kv(1)
-        load_qk(1, 0)
-        load_qk(1, 1)
-        load_kv(2)
         sink_bf = const.tile([P, H], BF16, name="sink_bf")
         nc.scalar.dma_start(out=sink_bf[:], in_=attn_sink.partition_broadcast(P))
+        load_qk(0, 0, by_head=True)
+        load_qk(0, 1)
+        load_qk(1, 0)
+        load_qk(1, 1)
+        for half in range(W_HALVES):
+            load_w(half)
+        load_kv(0)
 
         ident_bf = const.tile([P, P], BF16, name="ident_bf")
         make_identity(nc, ident_bf[:])
@@ -272,54 +311,62 @@ def tile_attention_pa_t_kernel(tc, q, k1, key_values_input, Wv1, attn_sink, out)
         neg_sink = const.tile([P, H], F32, name="neg_sink")
         nc.vector.tensor_copy(out=sink_f32[:], in_=sink_bf[:])
         nc.vector.tensor_scalar_mul(out=neg_sink[:], in0=sink_f32[:], scalar1=-1.0)
-        w_grouped = grouped.tile([P, DM, PACK], BF16, tag="v_grouped", name="w_grouped", align_bytes=64)
         w_codes = const.tile([P, DM], U32, name="w_codes", align_bytes=64)
         w_scales = const.tile([P, DM], U8, name="w_scales", align_bytes=64)
         turn_qk(0)
+        turn_qk(1)
 
         one_each = (nc.vector.tensor_copy, nc.scalar.copy)
-        both_vector = (nc.vector.tensor_copy, nc.vector.tensor_copy)
-        for g in range(GROUPS):
-            first = g * GROUP
-            kv_first, kv_end = (0, KV_FIRST) if g == 0 else (KV_FIRST, B)
-            for n in range(GROUP):
-                u = first + n
-                b, h = divmod(u, H)
-                if h == 0 and b + 2 < B:
-                    load_qk(b + 2, 0)
-                    load_qk(b + 2, 1)
-                if u + 1 < UNITS:
-                    turn_qk(u + 1)
-                begin_unit(u)
-                for a in range(TILES):
-                    scores(u, a)
-                denominators(u)
-                if n >= 1:
-                    turn_e(u - 1, one_each)
-                    reciprocals(u - 1)
-                if n >= 2:
-                    quantise_e(u - 2)
-                if g == 0 and n == LEAD_STEPS - 1:
-                    nc.vector.tensor_copy(out=w_grouped[:], in_=w_raw[:].rearrange("p t c -> p c t"))
-                    quantise(w_grouped, w_codes, w_scales)
-                kv_b = kv_first + n // KV_STEPS
-                if kv_b < kv_end and n % KV_STEPS == 0:
-                    turn_kv(kv_b)
-                    if kv_b + 3 < B:
-                        load_kv(kv_b + 3)
-                if kv_b < kv_end and n % KV_STEPS == 1:
-                    quantise_kv(kv_b)
-                if g == 0 and 0 <= n - LEAD_STEPS < LEAD // 2:
-                    project_values(2 * (n - LEAD_STEPS), nc.vector.tensor_copy)
-                    project_values(2 * (n - LEAD_STEPS) + 1, nc.scalar.copy)
+        two_scalar = (nc.scalar.copy, nc.scalar.copy)
+        for u in range(UNITS):
+            b, h = divmod(u, H)
+            if h % 2 == 0 and b + 2 < B:
+                load_qk(b + 2, h // 2)
+            begin_unit(u)
+            for a in range(TILES):
+                scores(u, a)
+                exponentials(u, a)
+            if h == H - 1:
+                denominators(b)
+            w_half, w_unit = divmod(u - W_STEP, PACK // W_PIECES)
+            if 0 <= w_half < W_HALVES:
+                for i in range(W_PIECES):
+                    group_w(w_half, W_PIECES * w_unit + i)
+                if W_PIECES * (w_unit + 1) == PACK:
+                    load_kv(1 + w_half)
+            if u >= 1:
+                turn_e(u - 1, one_each)
+                if h == 0:
+                    reciprocals(b - 1)
+            if u >= 2:
+                quantise_e(u - 2)
+            if u + 2 < UNITS:
+                turn_qk(u + 2)
+            if 0 <= w_half - 1 < W_HALVES and w_unit == 0:
+                quantise_w(w_half - 1)
+            kv_b, kv_unit = divmod(u - KV_STEP, KV_EVERY)
+            if 0 <= kv_b < B and kv_unit == 0:
+                turn_kv(kv_b)
+                if kv_b + 3 < B:
+                    load_kv(kv_b + 3)
+            if 0 <= kv_b < B and kv_unit == 1:
+                quantise_kv(kv_b)
+            lead = CHUNKS * (u - LEAD_STEP)
+            if 0 < lead <= LEAD:
+                quantise_v(u - LEAD_STEP - 1)
+            if 0 <= lead < LEAD:
+                project_values(lead, nc.vector.tensor_copy)
+                project_values(lead + 1, nc.scalar.copy)
 
-            last = first + GROUP - 1
-            turn_e(last, both_vector)
-            quantise_e(last - 1)
-            for n in range(GROUP):
-                for half in range(2):
-                    attend(first + n, half)
-                    project_values(LEAD + 2 * GROUP * g + 2 * n + half, nc.vector.tensor_copy)
-                if n == 0:
-                    quantise_e(last)
-                    reciprocals(last)
+        turn_e(UNITS - 1, one_each)
+        quantise_e(UNITS - 2)
+        for u in range(UNITS):
+            for half in range(2):
+                attend(u, half)
+                chunk = LEAD + CHUNKS * u + half
+                project_values(chunk, nc.vector.tensor_copy)
+                if half == 0:
+                    quantise_v(u + LEAD // CHUNKS - 1)
+            if u == 0:
+                quantise_e(UNITS - 1)
+                reciprocals(B - 1)

@@ -45,12 +45,14 @@ def tile_attention_pa_t_kernel(tc, q, k1, key_values_input, Wv1, attn_sink, out)
         turned_qk = stack.enter_context(tc.tile_pool(name="turned_qk", bufs=3))
         e_pool = stack.enter_context(tc.tile_pool(name="e_pool", bufs=3))
         stats = stack.enter_context(tc.tile_pool(name="stats", bufs=3))
-        grouped = stack.enter_context(tc.tile_pool(name="grouped", bufs=2))
+        e_grouping = stack.enter_context(tc.tile_pool(name="e_grouping", bufs=3))
+        v_grouping = stack.enter_context(tc.tile_pool(name="v_grouping", bufs=3))
+        kv_grouping = stack.enter_context(tc.tile_pool(name="kv_grouping", bufs=2))
         e_mx = stack.enter_context(tc.tile_pool(name="e_mx", bufs=UNITS))
         kept_stats = stack.enter_context(tc.tile_pool(name="kept_stats", bufs=B))
         kv_mx = stack.enter_context(tc.tile_pool(name="kv_mx", bufs=B))
         v_mx = stack.enter_context(tc.tile_pool(name="v_mx", bufs=LEAD // CHUNKS + 2))
-        results = stack.enter_context(tc.tile_pool(name="results", bufs=12))
+        results = stack.enter_context(tc.tile_pool(name="results", bufs=6))
         ps_s = stack.enter_context(tc.psum_pool(name="ps_s", bufs=4))
         ps_x = stack.enter_context(tc.psum_pool(name="ps_x", bufs=4))
 
@@ -60,6 +62,7 @@ def tile_attention_pa_t_kernel(tc, q, k1, key_values_input, Wv1, attn_sink, out)
         w_grouped = {}
         v_grouped, v_codes, v_scales = {}, {}, {}
         qkT, e_sb, e_grouped, e_codes, e_scales = {}, {}, {}, {}, {}
+        ys = {}
         s_banks = {}
         row_max, neg_max, row_sum, den, rden = {}, {}, {}, {}, {}
 
@@ -115,7 +118,7 @@ def tile_attention_pa_t_kernel(tc, q, k1, key_values_input, Wv1, attn_sink, out)
 
         def group_w(half, piece):
             if piece == 0:
-                w_grouped[half] = grouped.tile([P, N, PACK], BF16, tag="kv_grouped", name="w_grouped", align_bytes=64)
+                w_grouped[half] = kv_grouping.tile([P, N, PACK], BF16, tag="kv_grouped", name="w_grouped", align_bytes=64)
             cols = slice(piece * P, (piece + 1) * P)
             nc.gpsimd.tensor_scalar(
                 out=w_grouped[half][:, cols, :],
@@ -131,7 +134,7 @@ def tile_attention_pa_t_kernel(tc, q, k1, key_values_input, Wv1, attn_sink, out)
             quantise(w_grouped[half], w_codes[:, cols], w_scales[:, cols])
 
         def turn_kv(b):
-            kv_grouped[b] = grouped.tile([P, N, PACK], BF16, tag="kv_grouped", name="kv_grouped", align_bytes=64)
+            kv_grouped[b] = kv_grouping.tile([P, N, PACK], BF16, tag="kv_grouped", name="kv_grouped", align_bytes=64)
             regroup_by_transposes(raw[b][:].bitcast(F32), kv_grouped[b], one_each)
 
         def quantise_kv(b):
@@ -145,7 +148,7 @@ def tile_attention_pa_t_kernel(tc, q, k1, key_values_input, Wv1, attn_sink, out)
                 return
             b, h = divmod(u, H)
             if c == 0:
-                v_grouped[u] = grouped.tile([P, DV, PACK], BF16, name="v_grouped", align_bytes=64)
+                v_grouped[u] = v_grouping.tile([P, DV, PACK], BF16, name="v_grouped", align_bytes=64)
             cols = slice(h * DV + c * P, h * DV + (c + 1) * P)
             v_ps = ps_s.tile([P, PACK, P], F32, tag="s", name="v_ps")
             for t in range(PACK):
@@ -246,7 +249,7 @@ def tile_attention_pa_t_kernel(tc, q, k1, key_values_input, Wv1, attn_sink, out)
             nc.vector.reciprocal(out=rden[b][:], in_=den[b][:])
 
         def turn_e(u, copies):
-            e_grouped[u] = grouped.tile([P, N, PACK], BF16, name="e_grouped", align_bytes=64)
+            e_grouped[u] = e_grouping.tile([P, N, PACK], BF16, name="e_grouped", align_bytes=64)
             regroup_by_transposes(e_sb[u][:].bitcast(F32), e_grouped[u], copies)
 
         def quantise_e(u):
@@ -268,14 +271,20 @@ def tile_attention_pa_t_kernel(tc, q, k1, key_values_input, Wv1, attn_sink, out)
                     start=True,
                     stop=True,
                 )
-            y = results.tile([P, 2, DV], F32, name="y")
+            if half == 0:
+                ys[u] = results.tile([P, TILES, DV], F32, name="y")
+            y = ys[u][:, 2 * half : 2 * half + 2, :]
             for r in range(2):
                 a = 2 * half + r
                 nc.scalar.activation(
                     out=y[:, r, :], in_=o_ps[:, r, :], func=ACT.Silu, scale=rden[b][:, h, a : a + 1]
                 )
-            queries = slice(2 * half * P, (2 * half + 2) * P)
-            nc.sync.dma_start(out=out[b, h, queries, :].rearrange("(r p) c -> p r c", p=P), in_=y[:])
+            if u < UNITS - 1:
+                if half == 1:
+                    nc.sync.dma_start(out=out[b, h].rearrange("(r p) c -> p r c", p=P), in_=ys[u][:])
+            else:
+                queries = slice(2 * half * P, (2 * half + 2) * P)
+                nc.sync.dma_start(out=out[b, h, queries, :].rearrange("(r p) c -> p r c", p=P), in_=y)
 
         sink_bf = const.tile([P, H], BF16, name="sink_bf")
         nc.scalar.dma_start(out=sink_bf[:], in_=attn_sink.partition_broadcast(P))

@@ -48,13 +48,13 @@ def tile_attention_pa_t_kernel(tc, q, k1, key_values_input, Wv1, attn_sink, out)
         e_grouping = stack.enter_context(tc.tile_pool(name="e_grouping", bufs=3))
         v_grouping = stack.enter_context(tc.tile_pool(name="v_grouping", bufs=3))
         kv_grouping = stack.enter_context(tc.tile_pool(name="kv_grouping", bufs=2))
-        e_mx = stack.enter_context(tc.tile_pool(name="e_mx", bufs=UNITS))
+        e_mx = stack.enter_context(tc.tile_pool(name="e_mx", bufs=UNITS // 2))
         kept_stats = stack.enter_context(tc.tile_pool(name="kept_stats", bufs=B))
         kv_mx = stack.enter_context(tc.tile_pool(name="kv_mx", bufs=B))
         v_mx = stack.enter_context(tc.tile_pool(name="v_mx", bufs=LEAD // CHUNKS + 2))
         results = stack.enter_context(tc.tile_pool(name="results", bufs=6))
-        ps_s = stack.enter_context(tc.psum_pool(name="ps_s", bufs=4))
-        ps_x = stack.enter_context(tc.psum_pool(name="ps_x", bufs=4))
+        ps_s = stack.enter_context(tc.psum_pool(name="ps_s", bufs=5))
+        ps_x = stack.enter_context(tc.psum_pool(name="ps_x", bufs=3))
 
         q_sb, k_sb = {}, {}
         raw = {}
@@ -63,6 +63,7 @@ def tile_attention_pa_t_kernel(tc, q, k1, key_values_input, Wv1, attn_sink, out)
         v_grouped, v_codes, v_scales = {}, {}, {}
         qkT, e_sb, e_grouped, e_codes, e_scales = {}, {}, {}, {}, {}
         ys = {}
+        e_banks, qk_banks, o_banks = {}, {}, {}
         s_banks = {}
         row_max, neg_max, row_sum, den, rden = {}, {}, {}, {}, {}
 
@@ -93,10 +94,11 @@ def tile_attention_pa_t_kernel(tc, q, k1, key_values_input, Wv1, attn_sink, out)
                     in_=Wv1[256 * w : 256 * (w + 1), half * N : (half + 1) * N].rearrange("(p e) c -> p e c", e=2),
                 )
 
-        def regroup_by_transposes(words, target, copies):
-            target_words = target[:].bitcast(F32)
+        def regroup_by_transposes(words, pool, tag):
+            banks = []
             for half in range(2):
-                bank = ps_x.tile([P, 2, 2 * P], F32, tag="x", name="bank")
+                bank = pool.tile([P, 2, 2 * P], F32, tag=tag, name="bank")
+                banks.append(bank)
                 for w in range(2):
                     for r in range(2):
                         nc.tensor.transpose(
@@ -104,10 +106,13 @@ def tile_attention_pa_t_kernel(tc, q, k1, key_values_input, Wv1, attn_sink, out)
                             words[:, 2 * half + r, w * P : (w + 1) * P],
                             ident_f32[:],
                         )
-                copies[half](
-                    out=target_words[:, half * 2 * P : (half + 1) * 2 * P, :],
-                    in_=bank[:].rearrange("p w x -> p x w"),
-                )
+            return banks
+
+        def copy_bank(banks, target, half, copy):
+            copy(
+                out=target.bitcast(F32)[:, half * 2 * P : (half + 1) * 2 * P, :],
+                in_=banks[half][:].rearrange("p w x -> p x w"),
+            )
 
         def quantise(target, codes, scales):
             nc.vector.quantize_mx(
@@ -135,7 +140,9 @@ def tile_attention_pa_t_kernel(tc, q, k1, key_values_input, Wv1, attn_sink, out)
 
         def turn_kv(b):
             kv_grouped[b] = kv_grouping.tile([P, N, PACK], BF16, tag="kv_grouped", name="kv_grouped", align_bytes=64)
-            regroup_by_transposes(raw[b][:].bitcast(F32), kv_grouped[b], one_each)
+            banks = regroup_by_transposes(raw[b][:].bitcast(F32), ps_s, "s")
+            copy_bank(banks, kv_grouped[b][:], 0, nc.vector.tensor_copy)
+            copy_bank(banks, kv_grouped[b][:], 1, nc.scalar.copy)
 
         def quantise_kv(b):
             kv_codes[b] = kv_mx.tile([P, N], U32, name="kv_codes", align_bytes=64)
@@ -178,8 +185,11 @@ def tile_attention_pa_t_kernel(tc, q, k1, key_values_input, Wv1, attn_sink, out)
                 nc.tensor.transpose(qk_ps[:, 0, a * P : (a + 1) * P], q_sb[b, h // 2][:, h % 2, a, :], ident_bf[:])
             for a in range(TILES):
                 nc.tensor.transpose(qk_ps[:, 1, a * P : (a + 1) * P], k_sb[b, h // 2][:, h % 2, a, :], ident_bf[:])
+            qk_banks[u] = qk_ps
+
+        def copy_qk(u):
             qkT[u] = turned_qk.tile([P, 2, N], BF16, name="qkT")
-            nc.scalar.copy(out=qkT[u][:], in_=qk_ps[:])
+            nc.scalar.copy(out=qkT[u][:], in_=qk_banks[u][:])
 
         def begin_unit(u):
             b, h = divmod(u, H)
@@ -215,9 +225,12 @@ def tile_attention_pa_t_kernel(tc, q, k1, key_values_input, Wv1, attn_sink, out)
                     stop=True,
                 )
             nc.vector.tensor_reduce(out=row_max[b][:, h, a : a + 1], in_=s_ps[:], op=ALU.max, axis=AXIS.X)
+
+        def negate(u, a0, a1):
+            b, h = divmod(u, H)
             nc.gpsimd.tensor_scalar(
-                out=neg_max[b][:, h, a : a + 1],
-                in0=row_max[b][:, h, a : a + 1],
+                out=neg_max[b][:, h, a0:a1],
+                in0=row_max[b][:, h, a0:a1],
                 scalar1=-SCALE,
                 scalar2=neg_sink[:, h : h + 1],
                 op0=ALU.mult,
@@ -248,43 +261,54 @@ def tile_attention_pa_t_kernel(tc, q, k1, key_values_input, Wv1, attn_sink, out)
             rden[b] = kept_stats.tile([P, H, TILES], F32, name="rden")
             nc.vector.reciprocal(out=rden[b][:], in_=den[b][:])
 
-        def turn_e(u, copies):
-            e_grouped[u] = e_grouping.tile([P, N, PACK], BF16, name="e_grouped", align_bytes=64)
-            regroup_by_transposes(e_sb[u][:].bitcast(F32), e_grouped[u], copies)
+        def turn_e(u):
+            e_banks[u] = regroup_by_transposes(e_sb[u][:].bitcast(F32), ps_x, "x")
 
-        def quantise_e(u):
-            e_codes[u] = e_mx.tile([P, N], U32, name="e_codes", align_bytes=64)
-            e_scales[u] = e_mx.tile([P, N], U8, name="e_scales", align_bytes=64)
-            quantise(e_grouped[u], e_codes[u][:], e_scales[u][:])
+        def copy_e(u, half, copy):
+            pair, place = divmod(u, 2)
+            if pair not in e_grouped:
+                e_grouped[pair] = e_grouping.tile([P, 2 * N, PACK], BF16, name="e_grouped", align_bytes=64)
+            copy_bank(e_banks[u], e_grouped[pair][:, place * N : (place + 1) * N, :], half, copy)
 
-        def attend(u, half):
+        def quantise_e(pair):
+            e_codes[pair] = e_mx.tile([P, 2 * N], U32, name="e_codes", align_bytes=64)
+            e_scales[pair] = e_mx.tile([P, 2 * N], U8, name="e_scales", align_bytes=64)
+            quantise(e_grouped[pair], e_codes[pair][:], e_scales[pair][:])
+
+        def attend(u, halves=(0, 1)):
             b, h = divmod(u, H)
-            o_ps = ps_x.tile([P, 2, DV], F32, tag="x", name="o_ps")
-            for r in range(2):
-                rows = slice((2 * half + r) * P, (2 * half + r + 1) * P)
-                nc.tensor.matmul_mx(
-                    out=o_ps[:, r, :],
-                    lhsT=e_codes[u][:, rows].bitcast(FP8X4),
-                    lhsT_scale=e_scales[u][:, rows],
-                    rhs=v_codes[u][:].bitcast(FP8X4),
-                    rhs_scale=v_scales[u][:],
-                    start=True,
-                    stop=True,
-                )
-            if half == 0:
+            for half in halves:
+                o_ps = ps_x.tile([P, 2, DV], F32, tag="x", name="o_ps")
+                o_banks[u, half] = o_ps
+                for r in range(2):
+                    a = 2 * half + r
+                    column = ((u % 2) * TILES + a) * P
+                    rows = slice(column, column + P)
+                    nc.tensor.matmul_mx(
+                        out=o_ps[:, r, :],
+                        lhsT=e_codes[u // 2][:, rows].bitcast(FP8X4),
+                        lhsT_scale=e_scales[u // 2][:, rows],
+                        rhs=v_codes[u][:].bitcast(FP8X4),
+                        rhs_scale=v_scales[u][:],
+                        start=True,
+                        stop=True,
+                    )
+            if 0 in halves:
                 ys[u] = results.tile([P, TILES, DV], F32, name="y")
-            y = ys[u][:, 2 * half : 2 * half + 2, :]
-            for r in range(2):
-                a = 2 * half + r
-                nc.scalar.activation(
-                    out=y[:, r, :], in_=o_ps[:, r, :], func=ACT.Silu, scale=rden[b][:, h, a : a + 1]
-                )
-            if u < UNITS - 1:
-                if half == 1:
-                    nc.sync.dma_start(out=out[b, h].rearrange("(r p) c -> p r c", p=P), in_=ys[u][:])
-            else:
-                queries = slice(2 * half * P, (2 * half + 2) * P)
-                nc.sync.dma_start(out=out[b, h, queries, :].rearrange("(r p) c -> p r c", p=P), in_=y)
+            for half in reversed(halves):
+                for r in range(2):
+                    a = 2 * half + r
+                    nc.scalar.activation(
+                        out=ys[u][:, a, :], in_=o_banks[u, half][:, r, :], func=ACT.Silu, scale=rden[b][:, h, a : a + 1]
+                    )
+                if u == UNITS - 1:
+                    queries = slice(2 * half * P, (2 * half + 2) * P)
+                    nc.sync.dma_start(
+                        out=out[b, h, queries, :].rearrange("(r p) c -> p r c", p=P),
+                        in_=ys[u][:, 2 * half : 2 * half + 2, :],
+                    )
+            if u < UNITS - 1 and 1 in halves:
+                nc.sync.dma_start(out=out[b, h].rearrange("(r p) c -> p r c", p=P), in_=ys[u][:])
 
         sink_bf = const.tile([P, H], BF16, name="sink_bf")
         nc.scalar.dma_start(out=sink_bf[:], in_=attn_sink.partition_broadcast(P))
@@ -323,7 +347,9 @@ def tile_attention_pa_t_kernel(tc, q, k1, key_values_input, Wv1, attn_sink, out)
         w_codes = const.tile([P, DM], U32, name="w_codes", align_bytes=64)
         w_scales = const.tile([P, DM], U8, name="w_scales", align_bytes=64)
         turn_qk(0)
+        copy_qk(0)
         turn_qk(1)
+        copy_qk(1)
 
         one_each = (nc.vector.tensor_copy, nc.scalar.copy)
         two_scalar = (nc.scalar.copy, nc.scalar.copy)
@@ -332,9 +358,18 @@ def tile_attention_pa_t_kernel(tc, q, k1, key_values_input, Wv1, attn_sink, out)
             if h % 2 == 0 and b + 2 < B:
                 load_qk(b + 2, h // 2)
             begin_unit(u)
-            for a in range(TILES):
-                scores(u, a)
-                exponentials(u, a)
+            scores(u, 0)
+            negate(u, 0, 1)
+            exponentials(u, 0)
+            scores(u, 1)
+            negate(u, 1, 2)
+            exponentials(u, 1)
+            scores(u, 2)
+            negate(u, 2, 3)
+            exponentials(u, 2)
+            scores(u, 3)
+            negate(u, 3, 4)
+            exponentials(u, 3)
             if h == H - 1:
                 denominators(b)
             w_half, w_unit = divmod(u - W_STEP, PACK // W_PIECES)
@@ -344,13 +379,19 @@ def tile_attention_pa_t_kernel(tc, q, k1, key_values_input, Wv1, attn_sink, out)
                 if W_PIECES * (w_unit + 1) == PACK:
                     load_kv(1 + w_half)
             if u >= 1:
-                turn_e(u - 1, one_each)
-                if h == 0:
-                    reciprocals(b - 1)
-            if u >= 2:
-                quantise_e(u - 2)
+                turn_e(u - 1)
+            if u >= 1:
+                copy_e(u - 1, 0, nc.vector.tensor_copy)
             if u + 2 < UNITS:
                 turn_qk(u + 2)
+            if u + 2 < UNITS:
+                copy_qk(u + 2)
+            if u >= 1:
+                copy_e(u - 1, 1, nc.scalar.copy)
+            if u >= 1 and h == 0:
+                reciprocals(b - 1)
+            if u >= 3 and u % 2 == 1:
+                quantise_e((u - 3) // 2)
             if 0 <= w_half - 1 < W_HALVES and w_unit == 0:
                 quantise_w(w_half - 1)
             kv_b, kv_unit = divmod(u - KV_STEP, KV_EVERY)
@@ -367,15 +408,16 @@ def tile_attention_pa_t_kernel(tc, q, k1, key_values_input, Wv1, attn_sink, out)
                 project_values(lead, nc.vector.tensor_copy)
                 project_values(lead + 1, nc.scalar.copy)
 
-        turn_e(UNITS - 1, one_each)
-        quantise_e(UNITS - 2)
+        turn_e(UNITS - 1)
+        copy_e(UNITS - 1, 0, nc.vector.tensor_copy)
+        copy_e(UNITS - 1, 1, nc.scalar.copy)
         for u in range(UNITS):
-            for half in range(2):
-                attend(u, half)
-                chunk = LEAD + CHUNKS * u + half
-                project_values(chunk, nc.vector.tensor_copy)
-                if half == 0:
-                    quantise_v(u + LEAD // CHUNKS - 1)
+            chunk = LEAD + CHUNKS * u
+            attend(u, (0,))
+            project_values(chunk, nc.vector.tensor_copy)
+            quantise_v(u + LEAD // CHUNKS - 1)
+            attend(u, (1,))
+            project_values(chunk + 1, nc.scalar.copy if u % 8 == 0 else nc.vector.tensor_copy)
             if u == 0:
-                quantise_e(UNITS - 1)
+                quantise_e(UNITS // 2 - 1)
                 reciprocals(B - 1)

@@ -28,6 +28,7 @@ KV_STEP = 7
 KV_EVERY = 3
 LEAD = 6
 LEAD_STEP = 29
+WARM_UPS = 4
 SCALE = DH**-0.5
 NEG = -3.4028234663852886e38
 
@@ -73,7 +74,7 @@ def tile_attention_pa_t_kernel(tc, q, k1, key_values_input, Wv1, attn_sink, out)
             step = 1 if by_head else 2
             for j in range(0, 2, step):
                 heads = slice(2 * pair + j, 2 * pair + j + step)
-                for source, target in ((q, q_sb), (k1, k_sb)):
+                for source, target in ((k1, k_sb), (q, q_sb)):
                     nc.sync.dma_start(
                         out=target[b, pair][:, j : j + step],
                         in_=source[b, heads].rearrange("h (a p) d -> p h a d", p=P),
@@ -191,6 +192,21 @@ def tile_attention_pa_t_kernel(tc, q, k1, key_values_input, Wv1, attn_sink, out)
             qkT[u] = turned_qk.tile([P, 2, N], BF16, name="qkT")
             nc.scalar.copy(out=qkT[u][:], in_=qk_banks[u][:])
 
+        def first_unit():
+            qkT[0] = turned_qk.tile([P, 2, N], BF16, name="qkT")
+            for i, source, tiles, copy in (
+                (1, k_sb, range(TILES), nc.scalar.copy),
+                (0, q_sb, range(1), nc.vector.tensor_copy),
+                (0, q_sb, range(1, TILES), nc.vector.tensor_copy),
+            ):
+                bank = ps_x.tile([P, N], BF16, tag="x", name="bank")
+                for a in tiles:
+                    nc.tensor.matmul(
+                        bank[:, a * P : (a + 1) * P], lhsT=source[0, 0][:, 0, a, :], rhs=ident_bf[:], start=True, stop=True
+                    )
+                columns = slice(tiles[0] * P, (tiles[-1] + 1) * P)
+                copy(out=qkT[0][:, i, columns], in_=bank[:, columns])
+
         def begin_unit(u):
             b, h = divmod(u, H)
             e_sb[u] = e_pool.tile([P, TILES, N], BF16, name="e_sb")
@@ -301,15 +317,21 @@ def tile_attention_pa_t_kernel(tc, q, k1, key_values_input, Wv1, attn_sink, out)
                     nc.scalar.activation(
                         out=ys[u][:, a, :], in_=o_banks[u, half][:, r, :], func=ACT.Silu, scale=rden[b][:, h, a : a + 1]
                     )
+                    if u == UNITS - 1:
+                        nc.sync.dma_start(out=out[b, h, a * P : (a + 1) * P, :], in_=ys[u][:, a, :])
                 if u == UNITS - 1:
-                    queries = slice(2 * half * P, (2 * half + 2) * P)
-                    nc.sync.dma_start(
-                        out=out[b, h, queries, :].rearrange("(r p) c -> p r c", p=P),
-                        in_=ys[u][:, 2 * half : 2 * half + 2, :],
-                    )
-            if u < UNITS - 1 and 1 in halves:
-                nc.sync.dma_start(out=out[b, h].rearrange("(r p) c -> p r c", p=P), in_=ys[u][:])
+                    continue
+                queries = slice(2 * half * P, (2 * half + 2) * P)
+                nc.sync.dma_start(
+                    out=out[b, h, queries, :].rearrange("(r p) c -> p r c", p=P),
+                    in_=ys[u][:, 2 * half : 2 * half + 2, :],
+                )
 
+        idle = const.tile([P, N], BF16, name="idle")
+        nc.vector.memset(idle[:], 0.0)
+        idle_ps = ps_s.tile([P, N], F32, tag="s", name="idle_ps")
+        for i in range(WARM_UPS):
+            nc.tensor.matmul(idle_ps[:], lhsT=idle[:, :P], rhs=idle[:], start=True, stop=True)
         sink_bf = const.tile([P, H], BF16, name="sink_bf")
         nc.scalar.dma_start(out=sink_bf[:], in_=attn_sink.partition_broadcast(P))
         load_qk(0, 0, by_head=True)
@@ -342,12 +364,13 @@ def tile_attention_pa_t_kernel(tc, q, k1, key_values_input, Wv1, attn_sink, out)
         nc.scalar.activation(out=one[:], in_=zero[:], func=ACT.Exp)
         sink_f32 = const.tile([P, H], F32, name="sink_f32")
         neg_sink = const.tile([P, H], F32, name="neg_sink")
-        nc.vector.tensor_copy(out=sink_f32[:], in_=sink_bf[:])
-        nc.vector.tensor_scalar_mul(out=neg_sink[:], in0=sink_f32[:], scalar1=-1.0)
+        nc.gpsimd.tensor_copy(out=sink_f32[:], in_=sink_bf[:])
+        nc.gpsimd.tensor_scalar(
+            out=neg_sink[:], in0=sink_f32[:], scalar1=-1.0, scalar2=0.0, op0=ALU.mult, op1=ALU.add
+        )
         w_codes = const.tile([P, DM], U32, name="w_codes", align_bytes=64)
         w_scales = const.tile([P, DM], U8, name="w_scales", align_bytes=64)
-        turn_qk(0)
-        copy_qk(0)
+        first_unit()
         turn_qk(1)
         copy_qk(1)
 

@@ -74,11 +74,13 @@ def tile_attention_pa_t_kernel(tc, q, k1, key_values_input, Wv1, attn_sink, out)
             step = 1 if by_head else 2
             for j in range(0, 2, step):
                 heads = slice(2 * pair + j, 2 * pair + j + step)
-                for source, target in ((k1, k_sb), (q, q_sb)):
-                    nc.sync.dma_start(
-                        out=target[b, pair][:, j : j + step],
-                        in_=source[b, heads].rearrange("h (a p) d -> p h a d", p=P),
-                    )
+                nc.sync.dma_start(
+                    out=k_sb[b, pair][:, j : j + step], in_=k1[b, heads].rearrange("h (a p) d -> p h a d", p=P)
+                )
+                nc.sync.dma_start(
+                    out=q_sb[b, pair][:, j : j + step].rearrange("p h (g r) d -> p h g (r d)", r=2),
+                    in_=q[b, heads].rearrange("h (g p r) d -> p h g (r d)", p=P, r=2),
+                )
 
         def load_kv(b):
             raw[b] = kv_in.tile([P, PACK, DKV], BF16, name="raw")
@@ -222,23 +224,16 @@ def tile_attention_pa_t_kernel(tc, q, k1, key_values_input, Wv1, attn_sink, out)
             nc.tensor.matmul(
                 s_ps[:], lhsT=qkT[u][:, 0, a * P : (a + 1) * P], rhs=qkT[u][:, 1, :], start=True, stop=False
             )
-            last_tile = a == TILES - 1
-            nc.tensor.matmul(
-                s_ps[:, a * P : (a + 1) * P],
-                lhsT=mask_same[:],
-                rhs=ident_f32[:],
-                is_transpose=True,
-                start=False,
-                stop=last_tile,
-            )
-            if not last_tile:
+            g, r = divmod(a, 2)
+            touched = range(2 * g, min(2 * g + 3, TILES))
+            for t in touched:
                 nc.tensor.matmul(
-                    s_ps[:, (a + 1) * P : (a + 2) * P],
-                    lhsT=mask_next[:],
+                    s_ps[:, t * P : (t + 1) * P],
+                    lhsT=mask_tiles[t - 2 * g][:, r, :],
                     rhs=ident_f32[:],
                     is_transpose=True,
                     start=False,
-                    stop=True,
+                    stop=t == touched[-1],
                 )
             nc.vector.tensor_reduce(out=row_max[b][:, h, a : a + 1], in_=s_ps[:], op=ALU.max, axis=AXIS.X)
 
@@ -317,13 +312,9 @@ def tile_attention_pa_t_kernel(tc, q, k1, key_values_input, Wv1, attn_sink, out)
                     nc.scalar.activation(
                         out=ys[u][:, a, :], in_=o_banks[u, half][:, r, :], func=ACT.Silu, scale=rden[b][:, h, a : a + 1]
                     )
-                    if u == UNITS - 1:
-                        nc.sync.dma_start(out=out[b, h, a * P : (a + 1) * P, :], in_=ys[u][:, a, :])
-                if u == UNITS - 1:
-                    continue
                 queries = slice(2 * half * P, (2 * half + 2) * P)
                 nc.sync.dma_start(
-                    out=out[b, h, queries, :].rearrange("(r p) c -> p r c", p=P),
+                    out=out[b, h, queries, :].rearrange("(p r) c -> p r c", r=2),
                     in_=ys[u][:, 2 * half : 2 * half + 2, :],
                 )
 
@@ -346,18 +337,22 @@ def tile_attention_pa_t_kernel(tc, q, k1, key_values_input, Wv1, attn_sink, out)
         make_identity(nc, ident_bf[:])
         ident_f32 = const.tile([P, P], F32, name="ident_f32")
         make_identity(nc, ident_f32[:])
-        mask_same = const.tile([P, P], F32, name="mask_same")
-        nc.gpsimd.memset(mask_same[:], 0.0)
-        nc.gpsimd.affine_select(
-            out=mask_same[:], in_=mask_same[:], compare_op=ALU.is_ge, fill=NEG,
-            base=0, pattern=[[1, P]], channel_multiplier=-1,
-        )
-        mask_next = const.tile([P, P], F32, name="mask_next")
-        nc.gpsimd.memset(mask_next[:], 0.0)
-        nc.gpsimd.affine_select(
-            out=mask_next[:], in_=mask_next[:], compare_op=ALU.is_ge, fill=NEG,
-            base=-1, pattern=[[-1, P]], channel_multiplier=1,
-        )
+        mask_tiles = []
+        for name in ("mask_0", "mask_1", "mask_2"):
+            mask_tiles.append(const.tile([P, 2, P], F32, name=name))
+        for mask, value in zip(mask_tiles, (0.0, NEG, 0.0)):
+            nc.vector.memset(mask[:], value)
+
+        def keep_where(mask, base, step, otherwise):
+            nc.gpsimd.affine_select(
+                out=mask[:], in_=mask[:], compare_op=ALU.is_ge, fill=otherwise,
+                base=base, pattern=[[step, 2], [2 * step, P]], channel_multiplier=-step,
+            )
+
+        keep_where(mask_tiles[0], 0, 1, NEG)
+        keep_where(mask_tiles[1], 0, 1, 0.0)
+        keep_where(mask_tiles[1], P - 1, -1, 0.0)
+        keep_where(mask_tiles[2], P - 1, -1, NEG)
         zero = const.tile([P, 1], F32, name="zero")
         one = const.tile([P, 1], F32, name="one")
         nc.vector.memset(zero[:], 0.0)

@@ -45,12 +45,10 @@ def tile_attention_pa_t_kernel(tc, q, k1, key_values_input, Wv1, attn_sink, out)
         kv_in = stack.enter_context(tc.tile_pool(name="kv_in", bufs=3))
         turned_qk = stack.enter_context(tc.tile_pool(name="turned_qk", bufs=3))
         e_pool = stack.enter_context(tc.tile_pool(name="e_pool", bufs=3))
-        stats = stack.enter_context(tc.tile_pool(name="stats", bufs=3))
         e_grouping = stack.enter_context(tc.tile_pool(name="e_grouping", bufs=3))
         v_grouping = stack.enter_context(tc.tile_pool(name="v_grouping", bufs=3))
         kv_grouping = stack.enter_context(tc.tile_pool(name="kv_grouping", bufs=2))
         e_mx = stack.enter_context(tc.tile_pool(name="e_mx", bufs=UNITS // 2))
-        kept_stats = stack.enter_context(tc.tile_pool(name="kept_stats", bufs=B))
         kv_mx = stack.enter_context(tc.tile_pool(name="kv_mx", bufs=B))
         v_mx = stack.enter_context(tc.tile_pool(name="v_mx", bufs=LEAD // CHUNKS + 2))
         results = stack.enter_context(tc.tile_pool(name="results", bufs=6))
@@ -66,7 +64,6 @@ def tile_attention_pa_t_kernel(tc, q, k1, key_values_input, Wv1, attn_sink, out)
         ys = {}
         e_banks, qk_banks, o_banks = {}, {}, {}
         s_banks = {}
-        row_max, neg_max, row_sum, den, rden = {}, {}, {}, {}, {}
 
         def load_qk(b, pair, by_head=False):
             q_sb[b, pair] = qk_in.tile([P, 2, TILES, DH], BF16, name="q_sb")
@@ -212,10 +209,6 @@ def tile_attention_pa_t_kernel(tc, q, k1, key_values_input, Wv1, attn_sink, out)
         def begin_unit(u):
             b, h = divmod(u, H)
             e_sb[u] = e_pool.tile([P, TILES, N], BF16, name="e_sb")
-            if h == 0:
-                row_max[b] = stats.tile([P, H, TILES], F32, name="row_max")
-                neg_max[b] = stats.tile([P, H, TILES], F32, name="neg_max")
-                row_sum[b] = stats.tile([P, H, TILES], F32, name="row_sum")
 
         def scores(u, a):
             b, h = divmod(u, H)
@@ -235,13 +228,13 @@ def tile_attention_pa_t_kernel(tc, q, k1, key_values_input, Wv1, attn_sink, out)
                     start=False,
                     stop=t == touched[-1],
                 )
-            nc.vector.tensor_reduce(out=row_max[b][:, h, a : a + 1], in_=s_ps[:], op=ALU.max, axis=AXIS.X)
+            nc.vector.tensor_reduce(out=row_max[:, b, h, a : a + 1], in_=s_ps[:], op=ALU.max, axis=AXIS.X)
 
         def negate(u, a0, a1):
             b, h = divmod(u, H)
             nc.gpsimd.tensor_scalar(
-                out=neg_max[b][:, h, a0:a1],
-                in0=row_max[b][:, h, a0:a1],
+                out=neg_max[:, b, h, a0:a1],
+                in0=row_max[:, b, h, a0:a1],
                 scalar1=-SCALE,
                 scalar2=neg_sink[:, h : h + 1],
                 op0=ALU.mult,
@@ -254,23 +247,20 @@ def tile_attention_pa_t_kernel(tc, q, k1, key_values_input, Wv1, attn_sink, out)
                 out=e_sb[u][:, a, :],
                 in_=s_banks[u, a][:],
                 func=ACT.Exp,
-                bias=neg_max[b][:, h, a : a + 1],
+                bias=neg_max[:, b, h, a : a + 1],
                 scale=SCALE,
-                accum_out=row_sum[b][:, h, a : a + 1],
+                accum_out=row_sum[:, b, h, a : a + 1],
             )
 
-        def denominators(b):
-            sink_arg = stats.tile([P, H, TILES], F32, name="sink_arg")
-            sink_e = stats.tile([P, H, TILES], F32, name="sink_e")
-            den[b] = stats.tile([P, H, TILES], F32, name="den")
-            sinks = sink_f32[:].unsqueeze(2).broadcast_to([P, H, TILES])
-            nc.gpsimd.tensor_add(out=sink_arg[:], in0=neg_max[b][:], in1=sinks)
-            nc.scalar.activation(out=sink_e[:], in_=sink_arg[:], func=ACT.Exp)
-            nc.gpsimd.tensor_add(out=den[b][:], in0=row_sum[b][:], in1=sink_e[:])
+        def denominators(first, last):
+            group = slice(first, last)
+            sinks = sink_f32[:].unsqueeze(1).unsqueeze(3).broadcast_to([P, last - first, H, TILES])
+            nc.gpsimd.tensor_add(out=sink_arg[:, group], in0=neg_max[:, group], in1=sinks)
+            nc.scalar.activation(out=sink_e[:, group], in_=sink_arg[:, group], func=ACT.Exp)
+            nc.gpsimd.tensor_add(out=den[:, group], in0=row_sum[:, group], in1=sink_e[:, group])
 
-        def reciprocals(b):
-            rden[b] = kept_stats.tile([P, H, TILES], F32, name="rden")
-            nc.vector.reciprocal(out=rden[b][:], in_=den[b][:])
+        def reciprocals(first, last):
+            nc.vector.reciprocal(out=rden[:, first:last], in_=den[:, first:last])
 
         def turn_e(u):
             e_banks[u] = regroup_by_transposes(e_sb[u][:].bitcast(F32), ps_x, "x")
@@ -310,7 +300,7 @@ def tile_attention_pa_t_kernel(tc, q, k1, key_values_input, Wv1, attn_sink, out)
                 for r in range(2):
                     a = 2 * half + r
                     nc.scalar.activation(
-                        out=ys[u][:, a, :], in_=o_banks[u, half][:, r, :], func=ACT.Silu, scale=rden[b][:, h, a : a + 1]
+                        out=ys[u][:, a, :], in_=o_banks[u, half][:, r, :], func=ACT.Silu, scale=rden[:, b, h, a : a + 1]
                     )
                 queries = slice(2 * half * P, (2 * half + 2) * P)
                 nc.sync.dma_start(
@@ -363,6 +353,13 @@ def tile_attention_pa_t_kernel(tc, q, k1, key_values_input, Wv1, attn_sink, out)
         nc.gpsimd.tensor_scalar(
             out=neg_sink[:], in0=sink_f32[:], scalar1=-1.0, scalar2=0.0, op0=ALU.mult, op1=ALU.add
         )
+        row_max = const.tile([P, B, H, TILES], F32, name="row_max")
+        neg_max = const.tile([P, B, H, TILES], F32, name="neg_max")
+        row_sum = const.tile([P, B, H, TILES], F32, name="row_sum")
+        sink_arg = const.tile([P, B, H, TILES], F32, name="sink_arg")
+        sink_e = const.tile([P, B, H, TILES], F32, name="sink_e")
+        den = const.tile([P, B, H, TILES], F32, name="den")
+        rden = const.tile([P, B, H, TILES], F32, name="rden")
         w_codes = const.tile([P, DM], U32, name="w_codes", align_bytes=64)
         w_scales = const.tile([P, DM], U8, name="w_scales", align_bytes=64)
         first_unit()
@@ -388,8 +385,10 @@ def tile_attention_pa_t_kernel(tc, q, k1, key_values_input, Wv1, attn_sink, out)
             scores(u, 3)
             negate(u, 3, 4)
             exponentials(u, 3)
-            if h == H - 1:
-                denominators(b)
+            if u == UNITS - 2:
+                denominators(0, B - 1)
+            if u == UNITS - 1:
+                denominators(B - 1, B)
             w_half, w_unit = divmod(u - W_STEP, PACK // W_PIECES)
             if 0 <= w_half < W_HALVES:
                 for i in range(W_PIECES):
@@ -406,8 +405,8 @@ def tile_attention_pa_t_kernel(tc, q, k1, key_values_input, Wv1, attn_sink, out)
                 copy_qk(u + 2)
             if u >= 1:
                 copy_e(u - 1, 1, nc.scalar.copy)
-            if u >= 1 and h == 0:
-                reciprocals(b - 1)
+            if u == UNITS - 1:
+                reciprocals(0, B - 1)
             if u >= 3 and u % 2 == 1:
                 quantise_e((u - 3) // 2)
             if 0 <= w_half - 1 < W_HALVES and w_unit == 0:
@@ -438,4 +437,4 @@ def tile_attention_pa_t_kernel(tc, q, k1, key_values_input, Wv1, attn_sink, out)
             project_values(chunk + 1, nc.scalar.copy if u % 8 == 0 else nc.vector.tensor_copy)
             if u == 0:
                 quantise_e(UNITS // 2 - 1)
-                reciprocals(B - 1)
+                reciprocals(B - 1, B)

@@ -404,7 +404,7 @@ def tile_attention_pa_t_kernel(tc, q, k1, key_values_input, Wv1, attn_sink, out)
             if u + 2 < UNITS:
                 copy_qk(u + 2)
             if u >= 1:
-                copy_e(u - 1, 1, nc.scalar.copy)
+                copy_e(u - 1, 1, nc.vector.tensor_copy if u == 1 else nc.scalar.copy)
             if u == UNITS - 1:
                 reciprocals(0, B - 1)
             if u >= 3 and u % 2 == 1:

from contextlib import ExitStack

import concourse.mybir as mybir
from concourse.masks import make_identity

F32 = mybir.dt.float32
BF16 = mybir.dt.bfloat16
U32 = mybir.dt.uint32
U8 = mybir.dt.uint8
FP8X4 = mybir.dt.float8_e4m3fn_x4
ACT = mybir.ActivationFunctionType
ALU = mybir.AluOpType
AXIS = mybir.AxisListType

B, H, N, DH = 8, 4, 512, 128
DV = 256
DKV = 512
DM = H * DV
P = 128
PACK = 4
TILES = N // P
CHUNKS = DV // P
UNITS = B * H
W_HALVES = DM // N
W_PIECES = 2
W_STEP = 2
KV_STEP = 7
KV_EVERY = 3
LEAD = 6
LEAD_STEP = 29
WARM_UPS = 4
SCALE = DH**-0.5
NEG = -3.4028234663852886e38

FLOPS = 2 * B * N * DKV * DM + 2 * UNITS * N * N * DH + 2 * UNITS * N * N * DV


def tile_attention_pa_t_kernel(tc, q, k1, key_values_input, Wv1, attn_sink, out):
    nc = tc.nc
    with ExitStack() as stack:
        stack.enter_context(tc.manual_schedule())

        const = stack.enter_context(tc.tile_pool(name="const", bufs=1))
        qk_in = stack.enter_context(tc.tile_pool(name="qk_in", bufs=4))
        kv_in = stack.enter_context(tc.tile_pool(name="kv_in", bufs=3))
        turned_qk = stack.enter_context(tc.tile_pool(name="turned_qk", bufs=3))
        e_pool = stack.enter_context(tc.tile_pool(name="e_pool", bufs=3))
        e_grouping = stack.enter_context(tc.tile_pool(name="e_grouping", bufs=3))
        v_grouping = stack.enter_context(tc.tile_pool(name="v_grouping", bufs=3))
        kv_grouping = stack.enter_context(tc.tile_pool(name="kv_grouping", bufs=2))
        e_mx = stack.enter_context(tc.tile_pool(name="e_mx", bufs=UNITS // 2))
        kv_mx = stack.enter_context(tc.tile_pool(name="kv_mx", bufs=B))
        v_mx = stack.enter_context(tc.tile_pool(name="v_mx", bufs=LEAD // CHUNKS + 2))
        results = stack.enter_context(tc.tile_pool(name="results", bufs=6))
        ps_s = stack.enter_context(tc.psum_pool(name="ps_s", bufs=5))
        ps_x = stack.enter_context(tc.psum_pool(name="ps_x", bufs=3))

        q_sb, k_sb = {}, {}
        raw = {}
        kv_grouped, kv_codes, kv_scales = {}, {}, {}
        w_grouped = {}
        v_grouped, v_codes, v_scales = {}, {}, {}
        qkT, e_sb, e_grouped, e_codes, e_scales = {}, {}, {}, {}, {}
        ys = {}
        e_banks, qk_banks, o_banks = {}, {}, {}
        s_banks = {}

        def load_qk(b, pair, by_head=False):
            q_sb[b, pair] = qk_in.tile([P, 2, TILES, DH], BF16, name="q_sb")
            k_sb[b, pair] = qk_in.tile([P, 2, TILES, DH], BF16, name="k_sb")
            step = 1 if by_head else 2
            for j in range(0, 2, step):
                heads = slice(2 * pair + j, 2 * pair + j + step)
                nc.sync.dma_start(
                    out=k_sb[b, pair][:, j : j + step], in_=k1[b, heads].rearrange("h (a p) d -> p h a d", p=P)
                )
                nc.sync.dma_start(
                    out=q_sb[b, pair][:, j : j + step].rearrange("p h (g r) d -> p h g (r d)", r=2),
                    in_=q[b, heads].rearrange("h (g p r) d -> p h g (r d)", p=P, r=2),
                )

        def load_kv(b):
            raw[b] = kv_in.tile([P, PACK, DKV], BF16, name="raw")
            nc.sync.dma_start(
                out=raw[b][:].rearrange("p (w e) f -> p w (e f)", w=2),
                in_=key_values_input[b].rearrange("(w p e) f -> p w (e f)", w=2, e=2),
            )

        def load_w(half):
            raw["w", half] = kv_in.tile([P, PACK, N], BF16, name="raw")
            for w in range(2):
                nc.sync.dma_start(
                    out=raw["w", half][:, 2 * w : 2 * w + 2, :],
                    in_=Wv1[256 * w : 256 * (w + 1), half * N : (half + 1) * N].rearrange("(p e) c -> p e c", e=2),
                )

        def regroup_by_transposes(words, pool, tag):
            banks = []
            for half in range(2):
                bank = pool.tile([P, 2, 2 * P], F32, tag=tag, name="bank")
                banks.append(bank)
                for w in range(2):
                    for r in range(2):
                        nc.tensor.transpose(
                            bank[:, w, r * P : (r + 1) * P],
                            words[:, 2 * half + r, w * P : (w + 1) * P],
                            ident_f32[:],
                        )
            return banks

        def copy_bank(banks, target, half, copy):
            copy(
                out=target.bitcast(F32)[:, half * 2 * P : (half + 1) * 2 * P, :],
                in_=banks[half][:].rearrange("p w x -> p x w"),
            )

        def quantise(target, codes, scales):
            nc.vector.quantize_mx(
                out=codes.bitcast(FP8X4),
                scales=scales,
                in_=target[:].rearrange("p x t -> p (x t)"),
            )

        def group_w(half, piece):
            if piece == 0:
                w_grouped[half] = kv_grouping.tile([P, N, PACK], BF16, tag="kv_grouped", name="w_grouped", align_bytes=64)
            cols = slice(piece * P, (piece + 1) * P)
            nc.gpsimd.tensor_scalar(
                out=w_grouped[half][:, cols, :],
                in0=raw["w", half][:, :, cols].rearrange("p t c -> p c t"),
                scalar1=1.0,
                scalar2=0.0,
                op0=ALU.mult,
                op1=ALU.add,
            )

        def quantise_w(half):
            cols = slice(half * N, (half + 1) * N)
            quantise(w_grouped[half], w_codes[:, cols], w_scales[:, cols])

        def turn_kv(b):
            kv_grouped[b] = kv_grouping.tile([P, N, PACK], BF16, tag="kv_grouped", name="kv_grouped", align_bytes=64)
            banks = regroup_by_transposes(raw[b][:].bitcast(F32), ps_s, "s")
            copy_bank(banks, kv_grouped[b][:], 0, nc.vector.tensor_copy)
            copy_bank(banks, kv_grouped[b][:], 1, nc.scalar.copy)

        def quantise_kv(b):
            kv_codes[b] = kv_mx.tile([P, N], U32, name="kv_codes", align_bytes=64)
            kv_scales[b] = kv_mx.tile([P, N], U8, name="kv_scales", align_bytes=64)
            quantise(kv_grouped[b], kv_codes[b][:], kv_scales[b][:])

        def project_values(chunk, copy):
            u, c = divmod(chunk, CHUNKS)
            if u >= UNITS:
                return
            b, h = divmod(u, H)
            if c == 0:
                v_grouped[u] = v_grouping.tile([P, DV, PACK], BF16, name="v_grouped", align_bytes=64)
            cols = slice(h * DV + c * P, h * DV + (c + 1) * P)
            v_ps = ps_s.tile([P, PACK, P], F32, tag="s", name="v_ps")
            for t in range(PACK):
                keys = slice(t * P, (t + 1) * P)
                nc.tensor.matmul_mx(
                    out=v_ps[:, t, :],
                    lhsT=kv_codes[b][:, keys].bitcast(FP8X4),
                    lhsT_scale=kv_scales[b][:, keys],
                    rhs=w_codes[:, cols].bitcast(FP8X4),
                    rhs_scale=w_scales[:, cols],
                    start=True,
                    stop=True,
                )
            copy(out=v_grouped[u][:, c * P : (c + 1) * P, :], in_=v_ps[:].rearrange("p t c -> p c t"))

        def quantise_v(u):
            if u >= UNITS:
                return
            v_codes[u] = v_mx.tile([P, DV], U32, name="v_codes", align_bytes=64)
            v_scales[u] = v_mx.tile([P, DV], U8, name="v_scales", align_bytes=64)
            quantise(v_grouped[u], v_codes[u][:], v_scales[u][:])

        def turn_qk(u):
            b, h = divmod(u, H)
            qk_ps = ps_x.tile([P, 2, N], BF16, tag="x", name="qk_ps")
            for a in range(TILES):
                nc.tensor.transpose(qk_ps[:, 0, a * P : (a + 1) * P], q_sb[b, h // 2][:, h % 2, a, :], ident_bf[:])
            for a in range(TILES):
                nc.tensor.transpose(qk_ps[:, 1, a * P : (a + 1) * P], k_sb[b, h // 2][:, h % 2, a, :], ident_bf[:])
            qk_banks[u] = qk_ps

        def copy_qk(u):
            qkT[u] = turned_qk.tile([P, 2, N], BF16, name="qkT")
            nc.scalar.copy(out=qkT[u][:], in_=qk_banks[u][:])

        def first_unit():
            qkT[0] = turned_qk.tile([P, 2, N], BF16, name="qkT")
            for i, source, tiles, copy in (
                (1, k_sb, range(TILES), nc.scalar.copy),
                (0, q_sb, range(1), nc.vector.tensor_copy),
                (0, q_sb, range(1, TILES), nc.vector.tensor_copy),
            ):
                bank = ps_x.tile([P, N], BF16, tag="x", name="bank")
                for a in tiles:
                    nc.tensor.matmul(
                        bank[:, a * P : (a + 1) * P], lhsT=source[0, 0][:, 0, a, :], rhs=ident_bf[:], start=True, stop=True
                    )
                columns = slice(tiles[0] * P, (tiles[-1] + 1) * P)
                copy(out=qkT[0][:, i, columns], in_=bank[:, columns])

        def begin_unit(u):
            b, h = divmod(u, H)
            e_sb[u] = e_pool.tile([P, TILES, N], BF16, name="e_sb")

        def scores(u, a):
            b, h = divmod(u, H)
            s_ps = ps_s.tile([P, N], F32, tag="s", name="s_ps")
            s_banks[u, a] = s_ps
            nc.tensor.matmul(
                s_ps[:], lhsT=qkT[u][:, 0, a * P : (a + 1) * P], rhs=qkT[u][:, 1, :], start=True, stop=False
            )
            g, r = divmod(a, 2)
            touched = range(2 * g, min(2 * g + 3, TILES))
            for t in touched:
                nc.tensor.matmul(
                    s_ps[:, t * P : (t + 1) * P],
                    lhsT=mask_tiles[t - 2 * g][:, r, :],
                    rhs=ident_f32[:],
                    is_transpose=True,
                    start=False,
                    stop=t == touched[-1],
                )
            nc.vector.tensor_reduce(out=row_max[:, b, h, a : a + 1], in_=s_ps[:], op=ALU.max, axis=AXIS.X)

        def negate(u, a0, a1):
            b, h = divmod(u, H)
            nc.gpsimd.tensor_scalar(
                out=neg_max[:, b, h, a0:a1],
                in0=row_max[:, b, h, a0:a1],
                scalar1=-SCALE,
                scalar2=neg_sink[:, h : h + 1],
                op0=ALU.mult,
                op1=ALU.min,
            )

        def exponentials(u, a):
            b, h = divmod(u, H)
            nc.scalar.activation(
                out=e_sb[u][:, a, :],
                in_=s_banks[u, a][:],
                func=ACT.Exp,
                bias=neg_max[:, b, h, a : a + 1],
                scale=SCALE,
                accum_out=row_sum[:, b, h, a : a + 1],
            )

        def denominators(first, last):
            group = slice(first, last)
            sinks = sink_f32[:].unsqueeze(1).unsqueeze(3).broadcast_to([P, last - first, H, TILES])
            nc.gpsimd.tensor_add(out=sink_arg[:, group], in0=neg_max[:, group], in1=sinks)
            nc.scalar.activation(out=sink_e[:, group], in_=sink_arg[:, group], func=ACT.Exp)
            nc.gpsimd.tensor_add(out=den[:, group], in0=row_sum[:, group], in1=sink_e[:, group])

        def reciprocals(first, last):
            nc.vector.reciprocal(out=rden[:, first:last], in_=den[:, first:last])

        def turn_e(u):
            e_banks[u] = regroup_by_transposes(e_sb[u][:].bitcast(F32), ps_x, "x")

        def copy_e(u, half, copy):
            pair, place = divmod(u, 2)
            if pair not in e_grouped:
                e_grouped[pair] = e_grouping.tile([P, 2 * N, PACK], BF16, name="e_grouped", align_bytes=64)
            copy_bank(e_banks[u], e_grouped[pair][:, place * N : (place + 1) * N, :], half, copy)

        def quantise_e(pair):
            e_codes[pair] = e_mx.tile([P, 2 * N], U32, name="e_codes", align_bytes=64)
            e_scales[pair] = e_mx.tile([P, 2 * N], U8, name="e_scales", align_bytes=64)
            quantise(e_grouped[pair], e_codes[pair][:], e_scales[pair][:])

        def attend(u, halves=(0, 1)):
            b, h = divmod(u, H)
            for half in halves:
                o_ps = ps_x.tile([P, 2, DV], F32, tag="x", name="o_ps")
                o_banks[u, half] = o_ps
                for r in range(2):
                    a = 2 * half + r
                    column = ((u % 2) * TILES + a) * P
                    rows = slice(column, column + P)
                    nc.tensor.matmul_mx(
                        out=o_ps[:, r, :],
                        lhsT=e_codes[u // 2][:, rows].bitcast(FP8X4),
                        lhsT_scale=e_scales[u // 2][:, rows],
                        rhs=v_codes[u][:].bitcast(FP8X4),
                        rhs_scale=v_scales[u][:],
                        start=True,
                        stop=True,
                    )
            if 0 in halves:
                ys[u] = results.tile([P, TILES, DV], F32, name="y")
            for half in reversed(halves):
                for r in range(2):
                    a = 2 * half + r
                    nc.scalar.activation(
                        out=ys[u][:, a, :], in_=o_banks[u, half][:, r, :], func=ACT.Silu, scale=rden[:, b, h, a : a + 1]
                    )
                queries = slice(2 * half * P, (2 * half + 2) * P)
                nc.sync.dma_start(
                    out=out[b, h, queries, :].rearrange("(p r) c -> p r c", r=2),
                    in_=ys[u][:, 2 * half : 2 * half + 2, :],
                )

        idle = const.tile([P, N], BF16, name="idle")
        nc.vector.memset(idle[:], 0.0)
        idle_ps = ps_s.tile([P, N], F32, tag="s", name="idle_ps")
        for i in range(WARM_UPS):
            nc.tensor.matmul(idle_ps[:], lhsT=idle[:, :P], rhs=idle[:], start=True, stop=True)
        sink_bf = const.tile([P, H], BF16, name="sink_bf")
        nc.scalar.dma_start(out=sink_bf[:], in_=attn_sink.partition_broadcast(P))
        load_qk(0, 0, by_head=True)
        load_qk(0, 1)
        load_qk(1, 0)
        load_qk(1, 1)
        for half in range(W_HALVES):
            load_w(half)
        load_kv(0)

        ident_bf = const.tile([P, P], BF16, name="ident_bf")
        make_identity(nc, ident_bf[:])
        ident_f32 = const.tile([P, P], F32, name="ident_f32")
        make_identity(nc, ident_f32[:])
        mask_tiles = []
        for name in ("mask_0", "mask_1", "mask_2"):
            mask_tiles.append(const.tile([P, 2, P], F32, name=name))
        for mask, value in zip(mask_tiles, (0.0, NEG, 0.0)):
            nc.vector.memset(mask[:], value)

        def keep_where(mask, base, step, otherwise):
            nc.gpsimd.affine_select(
                out=mask[:], in_=mask[:], compare_op=ALU.is_ge, fill=otherwise,
                base=base, pattern=[[step, 2], [2 * step, P]], channel_multiplier=-step,
            )

        keep_where(mask_tiles[0], 0, 1, NEG)
        keep_where(mask_tiles[1], 0, 1, 0.0)
        keep_where(mask_tiles[1], P - 1, -1, 0.0)
        keep_where(mask_tiles[2], P - 1, -1, NEG)
        zero = const.tile([P, 1], F32, name="zero")
        one = const.tile([P, 1], F32, name="one")
        nc.vector.memset(zero[:], 0.0)
        nc.scalar.activation(out=one[:], in_=zero[:], func=ACT.Exp)
        sink_f32 = const.tile([P, H], F32, name="sink_f32")
        neg_sink = const.tile([P, H], F32, name="neg_sink")
        nc.gpsimd.tensor_copy(out=sink_f32[:], in_=sink_bf[:])
        nc.gpsimd.tensor_scalar(
            out=neg_sink[:], in0=sink_f32[:], scalar1=-1.0, scalar2=0.0, op0=ALU.mult, op1=ALU.add
        )
        row_max = const.tile([P, B, H, TILES], F32, name="row_max")
        neg_max = const.tile([P, B, H, TILES], F32, name="neg_max")
        row_sum = const.tile([P, B, H, TILES], F32, name="row_sum")
        sink_arg = const.tile([P, B, H, TILES], F32, name="sink_arg")
        sink_e = const.tile([P, B, H, TILES], F32, name="sink_e")
        den = const.tile([P, B, H, TILES], F32, name="den")
        rden = const.tile([P, B, H, TILES], F32, name="rden")
        w_codes = const.tile([P, DM], U32, name="w_codes", align_bytes=64)
        w_scales = const.tile([P, DM], U8, name="w_scales", align_bytes=64)
        first_unit()
        turn_qk(1)
        copy_qk(1)

        one_each = (nc.vector.tensor_copy, nc.scalar.copy)
        two_scalar = (nc.scalar.copy, nc.scalar.copy)
        for u in range(UNITS):
            b, h = divmod(u, H)
            if h % 2 == 0 and b + 2 < B:
                load_qk(b + 2, h // 2)
            begin_unit(u)
            scores(u, 0)
            negate(u, 0, 1)
            exponentials(u, 0)
            scores(u, 1)
            negate(u, 1, 2)
            exponentials(u, 1)
            scores(u, 2)
            negate(u, 2, 3)
            exponentials(u, 2)
            scores(u, 3)
            negate(u, 3, 4)
            exponentials(u, 3)
            if u == UNITS - 2:
                denominators(0, B - 1)
            if u == UNITS - 1:
                denominators(B - 1, B)
            w_half, w_unit = divmod(u - W_STEP, PACK // W_PIECES)
            if 0 <= w_half < W_HALVES:
                for i in range(W_PIECES):
                    group_w(w_half, W_PIECES * w_unit + i)
                if W_PIECES * (w_unit + 1) == PACK:
                    load_kv(1 + w_half)
            if u >= 1:
                turn_e(u - 1)
            if u >= 1:
                copy_e(u - 1, 0, nc.vector.tensor_copy)
            if u + 2 < UNITS:
                turn_qk(u + 2)
            if u + 2 < UNITS:
                copy_qk(u + 2)
            if u >= 1:
                copy_e(u - 1, 1, nc.vector.tensor_copy if u == 1 else nc.scalar.copy)
            if u == UNITS - 1:
                reciprocals(0, B - 1)
            if u >= 3 and u % 2 == 1:
                quantise_e((u - 3) // 2)
            if 0 <= w_half - 1 < W_HALVES and w_unit == 0:
                quantise_w(w_half - 1)
            kv_b, kv_unit = divmod(u - KV_STEP, KV_EVERY)
            if 0 <= kv_b < B and kv_unit == 0:
                turn_kv(kv_b)
                if kv_b + 3 < B:
                    load_kv(kv_b + 3)
            if 0 <= kv_b < B and kv_unit == 1:
                quantise_kv(kv_b)
            lead = CHUNKS * (u - LEAD_STEP)
            if 0 < lead <= LEAD:
                quantise_v(u - LEAD_STEP - 1)
            if 0 <= lead < LEAD:
                project_values(lead, nc.vector.tensor_copy)
                project_values(lead + 1, nc.scalar.copy)

        turn_e(UNITS - 1)
        copy_e(UNITS - 1, 0, nc.vector.tensor_copy)
        copy_e(UNITS - 1, 1, nc.scalar.copy)
        for u in range(UNITS):
            chunk = LEAD + CHUNKS * u
            attend(u, (0,))
            project_values(chunk, nc.vector.tensor_copy)
            quantise_v(u + LEAD // CHUNKS - 1)
            attend(u, (1,))
            project_values(chunk + 1, nc.scalar.copy if u % 8 == 0 else nc.vector.tensor_copy)
            if u == 0:
                quantise_e(UNITS // 2 - 1)
                reciprocals(B - 1, B)
